import numpy as np
import ml_dtypes


def mxq(x, axis, fmt="e4m3"):
    dtype, down = {"e4m3": (ml_dtypes.float8_e4m3fn, 7), "e5m2": (ml_dtypes.float8_e5m2, 14)}[fmt]
    v = np.moveaxis(np.asarray(x, np.float32).astype(ml_dtypes.bfloat16).astype(np.float64), axis, -1)
    blocks = v.reshape(v.shape[:-1] + (-1, 32))
    amax = np.abs(blocks).max(-1, keepdims=True)
    byte = np.maximum(np.where(amax > 0, np.frexp(amax)[1] - 1 + 127, 0) - down, 1)
    scale = np.exp2(byte - 127.0)
    codes = (blocks / scale).astype(np.float32).astype(dtype).astype(np.float64)
    return np.moveaxis((codes * scale).reshape(v.shape), -1, axis)


WIDE = False


def mx_kscale(k):
    if not WIDE:
        return np.ones(k)
    levels = np.array([10, -10, 5, -5, 0])
    if k % 512:
        return np.exp2(np.random.permutation(np.resize(levels, k // 32))).repeat(32)
    a = np.empty((k // 512, 16))
    for p in range(k // 512):
        a[p, :8] = np.random.permutation(np.resize(levels, 8))
        for g in range(8):
            far = levels[np.abs(levels - a[p, g]) >= 10]
            a[p, g + 8] = far[np.random.randint(len(far))]
    return np.exp2(a.ravel()).repeat(32)


BF16 = ml_dtypes.bfloat16


def bf(x):
    return np.asarray(x, np.float32).astype(BF16)


def f64(x):
    return np.asarray(x).astype(np.float64)


B, S, DIM, HEADS = 1, 512, 2048, 16
HD = DIM // HEADS
EPS = 1e-6


def rms_norm(x, g):
    var = np.mean(np.square(x), axis=-1, keepdims=True)
    return x * (1.0 / np.sqrt(var + EPS)) * g


def rope(x, cos, sin):
    x1, x2 = np.split(x, 2, axis=-1)
    rot = np.concatenate([-x2, x1], axis=-1)
    return x * cos[None, :, None, :] + rot * sin[None, :, None, :]


def setup_inputs():
    s = mx_kscale(DIM)
    return {
        "hidden_states": bf(np.random.standard_normal((B, S, DIM)) * s),
        "cos": bf(np.random.uniform(-1.0, 1.0, (S, HD))),
        "sin": bf(np.random.uniform(-1.0, 1.0, (S, HD))),
        "w_qk": bf(np.random.standard_normal((DIM + DIM, DIM)) / np.sqrt(DIM) / s[None, :]),
        "b_qk": bf(np.random.standard_normal(DIM + DIM) * 0.2),
        "g_q": bf(1.0 + 0.1 * np.random.standard_normal(DIM)),
        "g_k": bf(1.0 + 0.1 * np.random.standard_normal(DIM)),
    }


def reference(hidden_states, cos, sin, w_qk, b_qk, g_q, g_k):
    c, sn = f64(cos), f64(sin)
    qk = (mxq(f64(hidden_states), 2, "e4m3") @ mxq(f64(w_qk), 1, "e4m3").T) + f64(b_qk)
    q = rms_norm(qk[:, :, :DIM], f64(g_q)).reshape(B, S, HEADS, HD)
    k = rms_norm(qk[:, :, DIM:], f64(g_k)).reshape(B, S, HEADS, HD)
    return rope(q, c, sn), rope(k, c, sn)

@@ -1,0 +1,312 @@
+from contextlib import ExitStack
+
+import concourse.mybir as mybir
+from concourse.masks import make_identity
+
+F32 = mybir.dt.float32
+BF16 = mybir.dt.bfloat16
+U32 = mybir.dt.uint32
+U8 = mybir.dt.uint8
+FP8X4 = mybir.dt.float8_e4m3fn_x4
+ACT = mybir.ActivationFunctionType
+ALU = mybir.AluOpType
+AXIS = mybir.AxisListType
+
+P = 128
+TOKENS = 512
+TOKEN_TILES = TOKENS // P
+DIM = 2048
+HEAD_DIM = 128
+HALF_DIM = HEAD_DIM // 2
+HEADS = DIM // HEAD_DIM
+ALL_HEADS = 2 * HEADS
+K_PASS = 4 * P
+PASSES = DIM // K_PASS
+WORDS = K_PASS // 2
+PREFETCH = 6
+EPS = 1e-6
+
+FLOPS = 2 * TOKENS * 2 * DIM * DIM
+
+
+def tile_dynamicselfattention_pa_kernel(
+    tc, hidden_states, cos, sin, w_qk, b_qk, g_q, g_k, out_0, out_1
+):
+    nc = tc.nc
+    hidden_rows = hidden_states.flatten_outer_dims()
+    outs = [
+        out_0.rearrange("b s h d -> (b s) (h d)"),
+        out_1.rearrange("b s h d -> (b s) (h d)"),
+    ]
+
+    with ExitStack() as ctx:
+        const = ctx.enter_context(tc.tile_pool(name="const", bufs=1))
+        hidden_pool = ctx.enter_context(tc.tile_pool(name="hidden", bufs=TOKEN_TILES))
+        weight_pool = ctx.enter_context(tc.tile_pool(name="weight", bufs=PREFETCH + 2))
+        stage = ctx.enter_context(tc.tile_pool(name="stage", bufs=3))
+        result_pool = ctx.enter_context(tc.tile_pool(name="result", bufs=2))
+        flipped_pool = ctx.enter_context(tc.psum_pool(name="flipped", bufs=4))
+        acc_pool = ctx.enter_context(tc.psum_pool(name="acc", bufs=2))
+        back_pool = ctx.enter_context(tc.psum_pool(name="back", bufs=2))
+        ctx.enter_context(tc.manual_schedule())
+
+        weight_rows = {}
+        flipped_of = {}
+        grouped_of = {}
+        codes_of = {}
+        acc_of = {}
+        scaled_of = {}
+        square_sum = {}
+        rotated = {}
+        inv_rms_of = {}
+        total_of = {}
+
+        def load_weights(head):
+            w_rows = weight_pool.tile([P, DIM], BF16, name="w_rows")
+            nc.sync.dma_start(out=w_rows[:], in_=w_qk[head * P : (head + 1) * P, :])
+            weight_rows[head] = w_rows
+
+        vec_rows_bf = const.tile([P, P], BF16)
+        nc.vector.memset(vec_rows_bf[:], 0.0)
+        nc.scalar.dma_start(
+            out=vec_rows_bf[0:ALL_HEADS, :], in_=b_qk.rearrange("(h d) -> h d", d=HEAD_DIM)
+        )
+        nc.scalar.dma_start(
+            out=vec_rows_bf[ALL_HEADS : ALL_HEADS + HEADS, :],
+            in_=g_q.rearrange("(h d) -> h d", d=HEAD_DIM),
+        )
+        nc.scalar.dma_start(
+            out=vec_rows_bf[ALL_HEADS + HEADS : 2 * ALL_HEADS, :],
+            in_=g_k.rearrange("(h d) -> h d", d=HEAD_DIM),
+        )
+        cos_bf = const.tile([P, TOKEN_TILES, HEAD_DIM], BF16)
+        nc.scalar.dma_start(out=cos_bf[:], in_=cos.rearrange("(t p) d -> p t d", p=P))
+        sin_bf = const.tile([P, TOKEN_TILES, HEAD_DIM], BF16)
+        nc.scalar.dma_start(out=sin_bf[:], in_=sin.rearrange("(t p) d -> p t d", p=P))
+
+        hidden_tiles = []
+        for t in range(TOKEN_TILES):
+            h_rows = hidden_pool.tile([P, DIM], BF16, name="h_rows")
+            nc.sync.dma_start(out=h_rows[:], in_=hidden_rows[t * P : (t + 1) * P, :])
+            hidden_tiles.append(h_rows)
+        for head in range(PREFETCH):
+            load_weights(head)
+
+        ident = const.tile([P, P], F32)
+        make_identity(nc, ident[:])
+        eps_col = const.tile([P, 1], F32)
+        nc.vector.memset(eps_col[:], EPS)
+        warm = const.tile([P, 1], F32)
+        nc.scalar.activation(out=warm[:], in_=eps_col[:], func=ACT.Sqrt)
+
+        def transpose_words(rows_words, pair):
+            flipped = flipped_pool.tile([P, 2, 2, P], F32, name="flipped")
+            for g2 in range(2):
+                for u in range(2):
+                    first = (2 * pair + g2) * WORDS + u
+                    nc.tensor.transpose(
+                        flipped[:, g2, u, :], rows_words[:, first : first + WORDS - u : 2], ident[:]
+                    )
+            return flipped
+
+        def regroup(flipped, grouped_words, pair, copy):
+            copy(
+                out=grouped_words[:, 2 * pair : 2 * pair + 2, :, :],
+                in_=flipped[:].rearrange("p g u r -> p g r u"),
+            )
+
+        h_grouped = const.tile([P, PASSES * TOKENS * 4], BF16, align_bytes=64)
+        h_grouped_words = (
+            h_grouped[:].bitcast(F32).rearrange("p (g s u) -> p g s u", g=PASSES, u=2)
+        )
+        h_codes = const.tile([P, PASSES * TOKENS], U32, align_bytes=64)
+        h_scales = const.tile([P, PASSES * TOKENS], U8, align_bytes=64)
+        for t in range(TOKEN_TILES):
+            for pair, copy in enumerate([nc.scalar.copy, nc.vector.tensor_copy]):
+                flipped = transpose_words(hidden_tiles[t][:].bitcast(F32), pair)
+                regroup(flipped, h_grouped_words[:, :, t * P : (t + 1) * P, :], pair, copy)
+        for g in range(PASSES):
+            nc.vector.quantize_mx(
+                out=h_codes[:, g * TOKENS : (g + 1) * TOKENS].bitcast(FP8X4),
+                scales=h_scales[:, g * TOKENS : (g + 1) * TOKENS],
+                in_=h_grouped[:, g * TOKENS * 4 : (g + 1) * TOKENS * 4],
+            )
+
+        vec_rows = const.tile([P, P], F32)
+        nc.vector.tensor_copy(out=vec_rows[:], in_=vec_rows_bf[:])
+        vec_cols_ps = back_pool.tile([P, TOKEN_TILES, HEAD_DIM], F32, tag="back")
+        nc.tensor.transpose(vec_cols_ps[:, 0, :], vec_rows[:], ident[:])
+        vec_cols = const.tile([P, P], F32)
+        nc.vector.tensor_copy(out=vec_cols[:], in_=vec_cols_ps[:, 0, :])
+        bias_col = vec_cols[:, 0:ALL_HEADS]
+        gain_col = vec_cols[:, ALL_HEADS : 2 * ALL_HEADS]
+        gain_bias_col = const.tile([P, ALL_HEADS], F32)
+        nc.vector.tensor_tensor(out=gain_bias_col[:], in0=bias_col, in1=gain_col, op=ALU.mult)
+
+        cos_f = const.tile([P, TOKEN_TILES, HEAD_DIM], F32)
+        nc.vector.tensor_copy(out=cos_f[:], in_=cos_bf[:])
+        sin_signed = const.tile([P, TOKEN_TILES, HEAD_DIM], F32)
+        nc.vector.tensor_scalar(
+            out=sin_signed[:, :, 0:HALF_DIM],
+            in0=sin_bf[:, :, 0:HALF_DIM],
+            scalar1=-1.0,
+            scalar2=None,
+            op0=ALU.mult,
+        )
+        nc.vector.tensor_copy(
+            out=sin_signed[:, :, HALF_DIM:HEAD_DIM], in_=sin_bf[:, :, HALF_DIM:HEAD_DIM]
+        )
+
+        def flip(head, pair):
+            flipped_of[(head, pair)] = transpose_words(weight_rows[head][:].bitcast(F32), pair)
+
+        def regroup_weights(head):
+            w_grouped = stage.tile([P, PASSES * P * 4], BF16, name="w_grouped", align_bytes=64)
+            w_grouped_words = (
+                w_grouped[:].bitcast(F32).rearrange("p (g c u) -> p g c u", g=PASSES, u=2)
+            )
+            for pair in range(PASSES // 2):
+                regroup(flipped_of[(head, pair)], w_grouped_words, pair, nc.scalar.copy)
+            grouped_of[head] = w_grouped
+
+        def quantise(head):
+            w_codes = stage.tile([P, PASSES * P], U32, name="w_codes", align_bytes=64)
+            w_scales = stage.tile([P, PASSES * P], U8, name="w_scales", align_bytes=64)
+            nc.vector.quantize_mx(
+                out=w_codes[:].bitcast(FP8X4), scales=w_scales[:], in_=grouped_of[head][:]
+            )
+            codes_of[head] = (w_codes, w_scales)
+
+        def multiply(head, pair):
+            w_codes, w_scales = codes_of[head]
+            if pair == 0:
+                acc_of[head] = acc_pool.tile([P, TOKENS], F32, name="acc")
+            for g in range(2 * pair, 2 * pair + 2):
+                nc.tensor.matmul_mx(
+                    out=acc_of[head][:],
+                    lhsT=w_codes[:, g * P : (g + 1) * P].bitcast(FP8X4),
+                    lhsT_scale=w_scales[:, g * P : (g + 1) * P],
+                    rhs=h_codes[:, g * TOKENS : (g + 1) * TOKENS].bitcast(FP8X4),
+                    rhs_scale=h_scales[:, g * TOKENS : (g + 1) * TOKENS],
+                    start=(g == 0),
+                    stop=(g == PASSES - 1),
+                )
+
+        def bias_gain_square(head):
+            half, h = divmod(head, HEADS)
+            acc = acc_of[head]
+            scaled = stage.tile([P, TOKENS], F32, name="scaled")
+            nc.scalar.activation(
+                out=scaled[:],
+                in_=acc[:],
+                func=ACT.Identity,
+                bias=gain_bias_col[:, head : head + 1],
+                scale=gain_col[:, head : head + 1],
+            )
+            scaled_of[head] = scaled
+            if h == 0:
+                square = result_pool.tile([P, TOKENS], F32, name="square_sum")
+                square_sum[half] = square
+            else:
+                square = stage.tile([P, TOKENS], F32, name="square")
+            nc.scalar.activation(
+                out=square[:],
+                in_=acc[:],
+                func=ACT.Square,
+                bias=bias_col[:, head : head + 1],
+                scale=1.0,
+            )
+            if h > 0:
+                nc.gpsimd.tensor_tensor(
+                    out=square_sum[half][:], in0=square_sum[half][:], in1=square[:], op=ALU.add
+                )
+
+        def rotate(head):
+            half, h = divmod(head, HEADS)
+            if h == 0:
+                rotated[half] = result_pool.tile(
+                    [P, TOKEN_TILES, HEADS, HEAD_DIM], F32, name="rotated"
+                )
+            back = back_pool.tile([P, TOKEN_TILES, HEAD_DIM], F32, name="back")
+            for t in range(TOKEN_TILES):
+                nc.tensor.transpose(
+                    back[:, t, :], scaled_of[head][:, t * P : (t + 1) * P], ident[:]
+                )
+            straight = stage.tile([P, TOKEN_TILES, HEAD_DIM], F32, name="straight")
+            nc.vector.tensor_tensor(out=straight[:], in0=back[:], in1=cos_f[:], op=ALU.mult)
+            crossed = stage.tile([P, TOKEN_TILES, HEAD_DIM], F32, name="crossed")
+            nc.vector.tensor_tensor(
+                out=crossed[:, :, 0:HALF_DIM],
+                in0=back[:, :, HALF_DIM:HEAD_DIM],
+                in1=sin_signed[:, :, 0:HALF_DIM],
+                op=ALU.mult,
+            )
+            nc.vector.tensor_tensor(
+                out=crossed[:, :, HALF_DIM:HEAD_DIM],
+                in0=back[:, :, 0:HALF_DIM],
+                in1=sin_signed[:, :, HALF_DIM:HEAD_DIM],
+                op=ALU.mult,
+            )
+            nc.vector.tensor_tensor(
+                out=rotated[half][:, :, h, :], in0=straight[:], in1=crossed[:], op=ALU.add
+            )
+
+        def sum_squares(half):
+            sums_back = back_pool.tile([P, TOKEN_TILES, HEAD_DIM], F32, name="back")
+            for t in range(TOKEN_TILES):
+                nc.tensor.transpose(
+                    sums_back[:, t, :], square_sum[half][:, t * P : (t + 1) * P], ident[:]
+                )
+            total = stage.tile([P, TOKEN_TILES], F32, name="total")
+            nc.vector.tensor_reduce(out=total[:], in_=sums_back[:], axis=AXIS.X, op=ALU.add)
+            total_of[half] = total
+
+        def inverse_rms(half):
+            rms = stage.tile([P, TOKEN_TILES], F32, name="rms")
+            nc.scalar.activation(
+                out=rms[:],
+                in_=total_of[half][:],
+                func=ACT.Sqrt,
+                bias=eps_col[:, 0:1],
+                scale=1.0 / DIM,
+            )
+            inv_rms = stage.tile([P, TOKEN_TILES], F32, name="inv_rms")
+            nc.vector.reciprocal(out=inv_rms[:], in_=rms[:])
+            inv_rms_of[half] = inv_rms
+
+        def scale_and_store(half, t):
+            row = rotated[half][:, t, :, :].rearrange("p h d -> p (h d)")
+            nc.vector.tensor_scalar(
+                out=row,
+                in0=row,
+                scalar1=inv_rms_of[half][:, t : t + 1],
+                scalar2=None,
+                op0=ALU.mult,
+            )
+            nc.sync.dma_start(out=outs[half][t * P : (t + 1) * P, :], in_=row)
+
+        LAST_STAGE = 5
+        for step in range(ALL_HEADS + LAST_STAGE + TOKEN_TILES):
+            if step + PREFETCH < ALL_HEADS:
+                load_weights(step + PREFETCH)
+            if 0 <= step - 2 < ALL_HEADS:
+                quantise(step - 2)
+            if 0 <= step - LAST_STAGE < ALL_HEADS:
+                rotate(step - LAST_STAGE)
+            for half in range(2):
+                since = step - LAST_STAGE - (half * HEADS + HEADS - 1)
+                if since == 0:
+                    sum_squares(half)
+                if since == 1:
+                    inverse_rms(half)
+                if 1 <= since <= TOKEN_TILES:
+                    scale_and_store(half, since - 1)
+            if 0 <= step - 4 < ALL_HEADS:
+                bias_gain_square(step - 4)
+            if 0 <= step - 1 < ALL_HEADS:
+                regroup_weights(step - 1)
+            for pair in range(PASSES // 2):
+                if step < ALL_HEADS:
+                    flip(step, pair)
+                if 0 <= step - 3 < ALL_HEADS:
+                    multiply(step - 3, pair)

@@ -10,7 +10,6 @@ U8 = mybir.dt.uint8
 FP8X4 = mybir.dt.float8_e4m3fn_x4
 ACT = mybir.ActivationFunctionType
 ALU = mybir.AluOpType
-AXIS = mybir.AxisListType
 
 P = 128
 TOKENS = 512
@@ -22,11 +21,19 @@ HEADS = DIM // HEAD_DIM
 ALL_HEADS = 2 * HEADS
 K_PASS = 4 * P
 PASSES = DIM // K_PASS
+PAIRS = PASSES // 2
 WORDS = K_PASS // 2
-PREFETCH = 6
+PREFETCH = 5
 EPS = 1e-6
 
 FLOPS = 2 * TOKENS * 2 * DIM * DIM
+
+SECTIONS = [(0, 0, 4), (1, 0, 2), (1, 2, 2)]
+BANKS = [
+    (s, h, TOKEN_TILES // tiles)
+    for s, (half, first_tile, tiles) in enumerate(SECTIONS)
+    for h in range(0, HEADS, TOKEN_TILES // tiles)
+]
 
 
 def tile_dynamicselfattention_pa_kernel(
@@ -41,10 +48,10 @@ def tile_dynamicselfattention_pa_kernel(
 
     with ExitStack() as ctx:
         const = ctx.enter_context(tc.tile_pool(name="const", bufs=1))
-        hidden_pool = ctx.enter_context(tc.tile_pool(name="hidden", bufs=TOKEN_TILES))
-        weight_pool = ctx.enter_context(tc.tile_pool(name="weight", bufs=PREFETCH + 2))
+        rows_pool = ctx.enter_context(tc.tile_pool(name="rows", bufs=TOKEN_TILES + PREFETCH))
         stage = ctx.enter_context(tc.tile_pool(name="stage", bufs=3))
-        result_pool = ctx.enter_context(tc.tile_pool(name="result", bufs=2))
+        q_codes_pool = ctx.enter_context(tc.tile_pool(name="q_codes", bufs=7))
+        k_codes_pool = ctx.enter_context(tc.tile_pool(name="k_codes", bufs=HEADS))
         flipped_pool = ctx.enter_context(tc.psum_pool(name="flipped", bufs=4))
         acc_pool = ctx.enter_context(tc.psum_pool(name="acc", bufs=2))
         back_pool = ctx.enter_context(tc.psum_pool(name="back", bufs=2))
@@ -57,39 +64,41 @@ def tile_dynamicselfattention_pa_kernel(
         acc_of = {}
         scaled_of = {}
         square_sum = {}
+        last_square = {}
+        last_bank_of = {s: max(b for b in range(len(BANKS)) if BANKS[b][0] == s) for s in range(len(SECTIONS))}
         rotated = {}
         inv_rms_of = {}
-        total_of = {}
 
         def load_weights(head):
-            w_rows = weight_pool.tile([P, DIM], BF16, name="w_rows")
-            nc.sync.dma_start(out=w_rows[:], in_=w_qk[head * P : (head + 1) * P, :])
-            weight_rows[head] = w_rows
+            rows = rows_pool.tile([P, DIM], BF16, name="rows")
+            nc.sync.dma_start(out=rows[:], in_=w_qk[head * P : (head + 1) * P, :])
+            weight_rows[head] = rows
 
         vec_rows_bf = const.tile([P, P], BF16)
         nc.vector.memset(vec_rows_bf[:], 0.0)
-        nc.scalar.dma_start(
+        hidden_tiles = []
+        for t in range(TOKEN_TILES):
+            rows = rows_pool.tile([P, DIM], BF16, name="rows")
+            nc.sync.dma_start(out=rows[:], in_=hidden_rows[t * P : (t + 1) * P, :])
+            hidden_tiles.append(rows)
+        load_weights(0)
+        load_weights(1)
+        nc.sync.dma_start(
             out=vec_rows_bf[0:ALL_HEADS, :], in_=b_qk.rearrange("(h d) -> h d", d=HEAD_DIM)
         )
-        nc.scalar.dma_start(
+        nc.sync.dma_start(
             out=vec_rows_bf[ALL_HEADS : ALL_HEADS + HEADS, :],
             in_=g_q.rearrange("(h d) -> h d", d=HEAD_DIM),
         )
-        nc.scalar.dma_start(
+        nc.sync.dma_start(
             out=vec_rows_bf[ALL_HEADS + HEADS : 2 * ALL_HEADS, :],
             in_=g_k.rearrange("(h d) -> h d", d=HEAD_DIM),
         )
         cos_bf = const.tile([P, TOKEN_TILES, HEAD_DIM], BF16)
-        nc.scalar.dma_start(out=cos_bf[:], in_=cos.rearrange("(t p) d -> p t d", p=P))
+        nc.sync.dma_start(out=cos_bf[:], in_=cos.rearrange("(t p) d -> p t d", p=P))
         sin_bf = const.tile([P, TOKEN_TILES, HEAD_DIM], BF16)
-        nc.scalar.dma_start(out=sin_bf[:], in_=sin.rearrange("(t p) d -> p t d", p=P))
-
-        hidden_tiles = []
-        for t in range(TOKEN_TILES):
-            h_rows = hidden_pool.tile([P, DIM], BF16, name="h_rows")
-            nc.sync.dma_start(out=h_rows[:], in_=hidden_rows[t * P : (t + 1) * P, :])
-            hidden_tiles.append(h_rows)
-        for head in range(PREFETCH):
+        nc.sync.dma_start(out=sin_bf[:], in_=sin.rearrange("(t p) d -> p t d", p=P))
+        for head in range(2, PREFETCH):
             load_weights(head)
 
         ident = const.tile([P, P], F32)
@@ -109,11 +118,8 @@ def tile_dynamicselfattention_pa_kernel(
                     )
             return flipped
 
-        def regroup(flipped, grouped_words, pair, copy):
-            copy(
-                out=grouped_words[:, 2 * pair : 2 * pair + 2, :, :],
-                in_=flipped[:].rearrange("p g u r -> p g r u"),
-            )
+        def regroup(flipped, grouped_words, copy):
+            copy(out=grouped_words, in_=flipped[:].rearrange("p g u r -> p g r u"))
 
         h_grouped = const.tile([P, PASSES * TOKENS * 4], BF16, align_bytes=64)
         h_grouped_words = (
@@ -124,7 +130,11 @@ def tile_dynamicselfattention_pa_kernel(
         for t in range(TOKEN_TILES):
             for pair, copy in enumerate([nc.scalar.copy, nc.vector.tensor_copy]):
                 flipped = transpose_words(hidden_tiles[t][:].bitcast(F32), pair)
-                regroup(flipped, h_grouped_words[:, :, t * P : (t + 1) * P, :], pair, copy)
+                regroup(
+                    flipped,
+                    h_grouped_words[:, 2 * pair : 2 * pair + 2, t * P : (t + 1) * P, :],
+                    copy,
+                )
         for g in range(PASSES):
             nc.vector.quantize_mx(
                 out=h_codes[:, g * TOKENS : (g + 1) * TOKENS].bitcast(FP8X4),
@@ -133,180 +143,258 @@ def tile_dynamicselfattention_pa_kernel(
             )
 
         vec_rows = const.tile([P, P], F32)
-        nc.vector.tensor_copy(out=vec_rows[:], in_=vec_rows_bf[:])
-        vec_cols_ps = back_pool.tile([P, TOKEN_TILES, HEAD_DIM], F32, tag="back")
-        nc.tensor.transpose(vec_cols_ps[:, 0, :], vec_rows[:], ident[:])
         vec_cols = const.tile([P, P], F32)
-        nc.vector.tensor_copy(out=vec_cols[:], in_=vec_cols_ps[:, 0, :])
         bias_col = vec_cols[:, 0:ALL_HEADS]
         gain_col = vec_cols[:, ALL_HEADS : 2 * ALL_HEADS]
         gain_bias_col = const.tile([P, ALL_HEADS], F32)
-        nc.vector.tensor_tensor(out=gain_bias_col[:], in0=bias_col, in1=gain_col, op=ALU.mult)
-
         cos_f = const.tile([P, TOKEN_TILES, HEAD_DIM], F32)
-        nc.vector.tensor_copy(out=cos_f[:], in_=cos_bf[:])
         sin_signed = const.tile([P, TOKEN_TILES, HEAD_DIM], F32)
-        nc.vector.tensor_scalar(
-            out=sin_signed[:, :, 0:HALF_DIM],
-            in0=sin_bf[:, :, 0:HALF_DIM],
-            scalar1=-1.0,
-            scalar2=None,
-            op0=ALU.mult,
-        )
-        nc.vector.tensor_copy(
-            out=sin_signed[:, :, HALF_DIM:HEAD_DIM], in_=sin_bf[:, :, HALF_DIM:HEAD_DIM]
-        )
 
-        def flip(head, pair):
-            flipped_of[(head, pair)] = transpose_words(weight_rows[head][:].bitcast(F32), pair)
+        def make_bias_and_gain():
+            nc.vector.tensor_copy(out=vec_rows[:], in_=vec_rows_bf[:])
+            vec_cols_ps = back_pool.tile([P, TOKEN_TILES, HEAD_DIM], F32, name="back")
+            nc.tensor.transpose(vec_cols_ps[:, 0, :], vec_rows[:], ident[:])
+            nc.vector.tensor_copy(out=vec_cols[:], in_=vec_cols_ps[:, 0, :])
+            nc.vector.tensor_tensor(
+                out=gain_bias_col[:], in0=bias_col, in1=gain_col, op=ALU.mult
+            )
+
+        def make_rope_tables():
+            nc.vector.tensor_copy(out=cos_f[:], in_=cos_bf[:])
+            nc.vector.tensor_scalar(
+                out=sin_signed[:, :, 0:HALF_DIM],
+                in0=sin_bf[:, :, 0:HALF_DIM],
+                scalar1=-1.0,
+                scalar2=None,
+                op0=ALU.mult,
+            )
+            nc.vector.tensor_copy(
+                out=sin_signed[:, :, HALF_DIM:HEAD_DIM], in_=sin_bf[:, :, HALF_DIM:HEAD_DIM]
+            )
+
+        def flip(head):
+            flipped_of[head] = [
+                transpose_words(weight_rows[head][:].bitcast(F32), pair) for pair in range(PAIRS)
+            ]
 
         def regroup_weights(head):
             w_grouped = stage.tile([P, PASSES * P * 4], BF16, name="w_grouped", align_bytes=64)
             w_grouped_words = (
                 w_grouped[:].bitcast(F32).rearrange("p (g c u) -> p g c u", g=PASSES, u=2)
             )
-            for pair in range(PASSES // 2):
-                regroup(flipped_of[(head, pair)], w_grouped_words, pair, nc.scalar.copy)
+            for pair in range(PAIRS):
+                regroup(
+                    flipped_of[head][pair],
+                    w_grouped_words[:, 2 * pair : 2 * pair + 2, :, :],
+                    nc.scalar.copy,
+                )
             grouped_of[head] = w_grouped
 
         def quantise(head):
-            w_codes = stage.tile([P, PASSES * P], U32, name="w_codes", align_bytes=64)
-            w_scales = stage.tile([P, PASSES * P], U8, name="w_scales", align_bytes=64)
+            pool = q_codes_pool if head < HEADS else k_codes_pool
+            w_codes = pool.tile([P, PASSES * P], U32, name="w_codes", align_bytes=64)
+            w_scales = pool.tile([P, PASSES * P], U8, name="w_scales", align_bytes=64)
             nc.vector.quantize_mx(
                 out=w_codes[:].bitcast(FP8X4), scales=w_scales[:], in_=grouped_of[head][:]
             )
             codes_of[head] = (w_codes, w_scales)
 
-        def multiply(head, pair):
-            w_codes, w_scales = codes_of[head]
-            if pair == 0:
-                acc_of[head] = acc_pool.tile([P, TOKENS], F32, name="acc")
-            for g in range(2 * pair, 2 * pair + 2):
+        def pieces(bank):
+            s, h, heads = BANKS[bank]
+            half, first_tile, tiles = SECTIONS[s]
+            width = tiles * P
+            return [
+                (
+                    half * HEADS + h + i,
+                    slice(i * width, (i + 1) * width),
+                    first_tile * P,
+                )
+                for i in range(heads)
+            ]
+
+        def multiply(bank, part, parts):
+            if part == 0:
+                acc_of[bank] = acc_pool.tile([P, TOKENS], F32, name="acc")
+            calls = [(piece, g) for piece in pieces(bank) for g in range(PASSES)]
+            share = len(calls) // parts
+            for (head, columns, token), g in calls[part * share : (part + 1) * share]:
+                w_codes, w_scales = codes_of[head]
+                width = columns.stop - columns.start
+                first = g * TOKENS + token
                 nc.tensor.matmul_mx(
-                    out=acc_of[head][:],
+                    out=acc_of[bank][:, columns],
                     lhsT=w_codes[:, g * P : (g + 1) * P].bitcast(FP8X4),
                     lhsT_scale=w_scales[:, g * P : (g + 1) * P],
-                    rhs=h_codes[:, g * TOKENS : (g + 1) * TOKENS].bitcast(FP8X4),
-                    rhs_scale=h_scales[:, g * TOKENS : (g + 1) * TOKENS],
+                    rhs=h_codes[:, first : first + width].bitcast(FP8X4),
+                    rhs_scale=h_scales[:, first : first + width],
                     start=(g == 0),
                     stop=(g == PASSES - 1),
                 )
 
-        def bias_gain_square(head):
-            half, h = divmod(head, HEADS)
-            acc = acc_of[head]
+        def bias_gain_square(bank):
+            s, h, heads = BANKS[bank]
+            acc = acc_of[bank]
             scaled = stage.tile([P, TOKENS], F32, name="scaled")
-            nc.scalar.activation(
-                out=scaled[:],
-                in_=acc[:],
-                func=ACT.Identity,
-                bias=gain_bias_col[:, head : head + 1],
-                scale=gain_col[:, head : head + 1],
-            )
-            scaled_of[head] = scaled
+            for head, columns, token in pieces(bank):
+                nc.scalar.activation(
+                    out=scaled[:, columns],
+                    in_=acc[:, columns],
+                    func=ACT.Identity,
+                    bias=gain_bias_col[:, head : head + 1],
+                    scale=gain_col[:, head : head + 1],
+                )
+            scaled_of[bank] = scaled
             if h == 0:
-                square = result_pool.tile([P, TOKENS], F32, name="square_sum")
-                square_sum[half] = square
+                square = const.tile([P, TOKENS], F32, name="square_sum_%d" % s)
+                square_sum[s] = square
             else:
                 square = stage.tile([P, TOKENS], F32, name="square")
-            nc.scalar.activation(
-                out=square[:],
-                in_=acc[:],
-                func=ACT.Square,
-                bias=bias_col[:, head : head + 1],
-                scale=1.0,
-            )
-            if h > 0:
+            for head, columns, token in pieces(bank):
+                nc.scalar.activation(
+                    out=square[:, columns],
+                    in_=acc[:, columns],
+                    func=ACT.Square,
+                    bias=bias_col[:, head : head + 1],
+                    scale=1.0,
+                )
+            if bank == last_bank_of[s]:
+                last_square[s] = square
+            elif h > 0:
                 nc.gpsimd.tensor_tensor(
-                    out=square_sum[half][:], in0=square_sum[half][:], in1=square[:], op=ALU.add
+                    out=square_sum[s][:], in0=square_sum[s][:], in1=square[:], op=ALU.add
                 )
 
-        def rotate(head):
-            half, h = divmod(head, HEADS)
-            if h == 0:
-                rotated[half] = result_pool.tile(
-                    [P, TOKEN_TILES, HEADS, HEAD_DIM], F32, name="rotated"
-                )
+        def turn_back(bank):
             back = back_pool.tile([P, TOKEN_TILES, HEAD_DIM], F32, name="back")
-            for t in range(TOKEN_TILES):
+            for j in range(TOKEN_TILES):
                 nc.tensor.transpose(
-                    back[:, t, :], scaled_of[head][:, t * P : (t + 1) * P], ident[:]
+                    back[:, j, :], scaled_of[bank][:, j * P : (j + 1) * P], ident[:]
                 )
-            straight = stage.tile([P, TOKEN_TILES, HEAD_DIM], F32, name="straight")
-            nc.vector.tensor_tensor(out=straight[:], in0=back[:], in1=cos_f[:], op=ALU.mult)
-            crossed = stage.tile([P, TOKEN_TILES, HEAD_DIM], F32, name="crossed")
+            return back
+
+        def rotate(bank, back):
+            s, h, heads = BANKS[bank]
+            half, first_tile, tiles = SECTIONS[s]
+            if h == 0:
+                rotated[s] = const.tile([P, tiles, HEADS, HEAD_DIM], F32, name="rotated_%d" % s)
+            x = back[:].rearrange("p (i t) d -> p i t d", i=heads)
+            low, high = slice(0, HALF_DIM), slice(HALF_DIM, HEAD_DIM)
+            shape = [P, heads, tiles, HEAD_DIM]
+            half_shape = [P, heads, tiles, HALF_DIM]
+            these = slice(first_tile, first_tile + tiles)
+            straight = stage.tile(shape, F32, name="straight")
             nc.vector.tensor_tensor(
-                out=crossed[:, :, 0:HALF_DIM],
-                in0=back[:, :, HALF_DIM:HEAD_DIM],
-                in1=sin_signed[:, :, 0:HALF_DIM],
+                out=straight[:],
+                in0=x,
+                in1=cos_f[:, these, :].unsqueeze(1).to_broadcast(shape),
                 op=ALU.mult,
             )
+            crossed = stage.tile(shape, F32, name="crossed")
+            for to, source in ((low, high), (high, low)):
+                nc.vector.tensor_tensor(
+                    out=crossed[:, :, :, to],
+                    in0=x[:, :, :, source],
+                    in1=sin_signed[:, these, to].unsqueeze(1).to_broadcast(half_shape),
+                    op=ALU.mult,
+                )
             nc.vector.tensor_tensor(
-                out=crossed[:, :, HALF_DIM:HEAD_DIM],
-                in0=back[:, :, 0:HALF_DIM],
-                in1=sin_signed[:, :, HALF_DIM:HEAD_DIM],
-                op=ALU.mult,
-            )
-            nc.vector.tensor_tensor(
-                out=rotated[half][:, :, h, :], in0=straight[:], in1=crossed[:], op=ALU.add
+                out=rotated[s][:, :, h : h + heads, :].rearrange("p t i d -> p i t d"),
+                in0=straight[:],
+                in1=crossed[:],
+                op=ALU.add,
             )
 
-        def sum_squares(half):
+        def inverse_rms(s):
+            half, first_tile, tiles = SECTIONS[s]
             sums_back = back_pool.tile([P, TOKEN_TILES, HEAD_DIM], F32, name="back")
-            for t in range(TOKEN_TILES):
-                nc.tensor.transpose(
-                    sums_back[:, t, :], square_sum[half][:, t * P : (t + 1) * P], ident[:]
+            for j in range(TOKEN_TILES):
+                for squares, first in ((square_sum[s], True), (last_square[s], False)):
+                    nc.tensor.matmul(
+                        out=sums_back[:, j, :],
+                        lhsT=squares[:, j * P : (j + 1) * P],
+                        rhs=ident[:],
+                        is_transpose=True,
+                        start=first,
+                        stop=not first,
+                    )
+            total = const.tile([P, tiles], F32, name="total_%d" % s)
+            by_tile = sums_back[:].rearrange("p (i t) d -> p t i d", t=tiles)
+            unused = stage.tile([P, TOKEN_TILES // tiles, HEAD_DIM], F32, name="unused")
+            for t in range(tiles):
+                nc.scalar.activation(
+                    out=unused[:],
+                    in_=by_tile[:, t, :, :],
+                    func=ACT.Copy,
+                    accum_out=total[:, t : t + 1],
                 )
-            total = stage.tile([P, TOKEN_TILES], F32, name="total")
-            nc.vector.tensor_reduce(out=total[:], in_=sums_back[:], axis=AXIS.X, op=ALU.add)
-            total_of[half] = total
-
-        def inverse_rms(half):
-            rms = stage.tile([P, TOKEN_TILES], F32, name="rms")
+            rms = const.tile([P, tiles], F32, name="rms_%d" % s)
             nc.scalar.activation(
-                out=rms[:],
-                in_=total_of[half][:],
-                func=ACT.Sqrt,
-                bias=eps_col[:, 0:1],
-                scale=1.0 / DIM,
+                out=rms[:], in_=total[:], func=ACT.Sqrt, bias=eps_col[:, 0:1], scale=1.0 / DIM
             )
-            inv_rms = stage.tile([P, TOKEN_TILES], F32, name="inv_rms")
+            inv_rms = const.tile([P, tiles], F32, name="inv_rms_%d" % s)
             nc.vector.reciprocal(out=inv_rms[:], in_=rms[:])
-            inv_rms_of[half] = inv_rms
+            inv_rms_of[s] = inv_rms
 
-        def scale_and_store(half, t):
-            row = rotated[half][:, t, :, :].rearrange("p h d -> p (h d)")
-            nc.vector.tensor_scalar(
-                out=row,
-                in0=row,
-                scalar1=inv_rms_of[half][:, t : t + 1],
-                scalar2=None,
-                op0=ALU.mult,
-            )
-            nc.sync.dma_start(out=outs[half][t * P : (t + 1) * P, :], in_=row)
+        def scale_and_store(s, t, side):
+            half, first_tile, tiles = SECTIONS[s]
+            heads = slice(side * HEADS // 2, (side + 1) * HEADS // 2)
+            columns = slice(side * DIM // 2, (side + 1) * DIM // 2)
+            row = rotated[s][:, t, heads, :].rearrange("p h d -> p (h d)")
+            factor = inv_rms_of[s][:, t : t + 1]
+            if s == 1:
+                nc.scalar.activation(out=row, in_=row, func=ACT.Copy, scale=factor)
+            else:
+                nc.vector.tensor_scalar(
+                    out=row, in0=row, scalar1=factor, scalar2=None, op0=ALU.mult
+                )
+            token = (first_tile + t) * P
+            nc.sync.dma_start(out=outs[half][token : token + P, columns], in_=row)
 
-        LAST_STAGE = 5
-        for step in range(ALL_HEADS + LAST_STAGE + TOKEN_TILES):
-            if step + PREFETCH < ALL_HEADS:
-                load_weights(step + PREFETCH)
-            if 0 <= step - 2 < ALL_HEADS:
-                quantise(step - 2)
-            if 0 <= step - LAST_STAGE < ALL_HEADS:
-                rotate(step - LAST_STAGE)
-            for half in range(2):
-                since = step - LAST_STAGE - (half * HEADS + HEADS - 1)
-                if since == 0:
-                    sum_squares(half)
-                if since == 1:
-                    inverse_rms(half)
-                if 1 <= since <= TOKEN_TILES:
-                    scale_and_store(half, since - 1)
-            if 0 <= step - 4 < ALL_HEADS:
-                bias_gain_square(step - 4)
-            if 0 <= step - 1 < ALL_HEADS:
-                regroup_weights(step - 1)
-            for pair in range(PASSES // 2):
-                if step < ALL_HEADS:
-                    flip(step, pair)
-                if 0 <= step - 3 < ALL_HEADS:
-                    multiply(step - 3, pair)
+        LEAD = 3
+
+        def heads_ready(step):
+            return max(0, min(ALL_HEADS, (4 * (step + 1) + 2) // 3))
+
+        def heads_of(step):
+            return range(heads_ready(step - 1), heads_ready(step))
+
+        tail = []
+        for step in range(len(BANKS) + LEAD + 3):
+            for head in heads_of(step):
+                if head + PREFETCH < ALL_HEADS:
+                    load_weights(head + PREFETCH)
+            for head in heads_of(step - 1):
+                regroup_weights(head)
+            for head in heads_of(step - 2):
+                quantise(head)
+            bank = step - LEAD
+            turned = bank - 2
+            if 0 <= turned < len(BANKS):
+                back = turn_back(turned)
+            fresh = heads_of(step)
+            if 0 <= bank < len(BANKS):
+                parts = max(1, len(fresh))
+                for part in range(parts):
+                    multiply(bank, part, parts)
+                    if part < len(fresh):
+                        flip(fresh[part])
+            else:
+                for head in fresh:
+                    flip(head)
+            if 0 <= bank - 1 < len(BANKS):
+                bias_gain_square(bank - 1)
+            if 0 <= turned < len(BANKS):
+                rotate(turned, back)
+            if tail:
+                scale_and_store(*tail.pop(0))
+            for s, (half, first_tile, tiles) in enumerate(SECTIONS):
+                settle = 0 if s == len(SECTIONS) - 1 else 1
+                if turned == last_bank_of[s] + settle:
+                    inverse_rms(s)
+                    tail.extend((s, t, side) for t in range(tiles) for side in range(2))
+            if step == 2:
+                make_bias_and_gain()
+            if step == 3:
+                make_rope_tables()
+        for args in tail:
+            scale_and_store(*args)

@@ -23,18 +23,19 @@ K_PASS = 4 * P
 PASSES = DIM // K_PASS
 PAIRS = PASSES // 2
 WORDS = K_PASS // 2
-PREFETCH = 5
+PREFETCH = 6
+PARTS = 4
 EPS = 1e-6
 
 FLOPS = 2 * TOKENS * 2 * DIM * DIM
 
-SECTIONS = [(0, 0, 4), (1, 0, 2), (1, 2, 2)]
+SECTIONS = [(0, 0, 4), (1, 0, 3), (1, 3, 1)]
 BANKS = [
-    (s, h, TOKEN_TILES // tiles)
-    for s, (half, first_tile, tiles) in enumerate(SECTIONS)
-    for h in range(0, HEADS, TOKEN_TILES // tiles)
+    (s, h, heads)
+    for s, heads in enumerate((1, 1, 4))
+    for h in range(0, HEADS, heads)
 ]
-
+MX_WIDTHS = (512, 256, 128)
 
 def tile_dynamicselfattention_pa_kernel(
     tc, hidden_states, cos, sin, w_qk, b_qk, g_q, g_k, out_0, out_1
@@ -50,7 +51,7 @@ def tile_dynamicselfattention_pa_kernel(
         const = ctx.enter_context(tc.tile_pool(name="const", bufs=1))
         rows_pool = ctx.enter_context(tc.tile_pool(name="rows", bufs=TOKEN_TILES + PREFETCH))
         stage = ctx.enter_context(tc.tile_pool(name="stage", bufs=3))
-        q_codes_pool = ctx.enter_context(tc.tile_pool(name="q_codes", bufs=7))
+        q_codes_pool = ctx.enter_context(tc.tile_pool(name="q_codes", bufs=3))
         k_codes_pool = ctx.enter_context(tc.tile_pool(name="k_codes", bufs=HEADS))
         flipped_pool = ctx.enter_context(tc.psum_pool(name="flipped", bufs=4))
         acc_pool = ctx.enter_context(tc.psum_pool(name="acc", bufs=2))
@@ -65,9 +66,13 @@ def tile_dynamicselfattention_pa_kernel(
         scaled_of = {}
         square_sum = {}
         last_square = {}
+        square_of = {}
+        LAST = len(SECTIONS) - 1
         last_bank_of = {s: max(b for b in range(len(BANKS)) if BANKS[b][0] == s) for s in range(len(SECTIONS))}
+        products_of = {}
         rotated = {}
         inv_rms_of = {}
+        rms_of = {}
 
         def load_weights(head):
             rows = rows_pool.tile([P, DIM], BF16, name="rows")
@@ -204,38 +209,36 @@ def tile_dynamicselfattention_pa_kernel(
             half, first_tile, tiles = SECTIONS[s]
             width = tiles * P
             return [
-                (
-                    half * HEADS + h + i,
-                    slice(i * width, (i + 1) * width),
-                    first_tile * P,
-                )
-                for i in range(heads)
+                (half * HEADS + h + i, slice(i * width, (i + 1) * width)) for i in range(heads)
             ]
 
-        def multiply(bank, part, parts):
-            if part == 0:
-                acc_of[bank] = acc_pool.tile([P, TOKENS], F32, name="acc")
-            calls = [(piece, g) for piece in pieces(bank) for g in range(PASSES)]
-            share = len(calls) // parts
-            for (head, columns, token), g in calls[part * share : (part + 1) * share]:
+        def multiply(bank):
+            half, first_tile, tiles = SECTIONS[BANKS[bank][0]]
+            acc_of[bank] = acc_pool.tile([P, TOKENS], F32, name="acc")
+            for head, columns in pieces(bank):
                 w_codes, w_scales = codes_of[head]
-                width = columns.stop - columns.start
-                first = g * TOKENS + token
-                nc.tensor.matmul_mx(
-                    out=acc_of[bank][:, columns],
-                    lhsT=w_codes[:, g * P : (g + 1) * P].bitcast(FP8X4),
-                    lhsT_scale=w_scales[:, g * P : (g + 1) * P],
-                    rhs=h_codes[:, first : first + width].bitcast(FP8X4),
-                    rhs_scale=h_scales[:, first : first + width],
-                    start=(g == 0),
-                    stop=(g == PASSES - 1),
-                )
+                done = 0
+                while done < tiles * P:
+                    width = max(w for w in MX_WIDTHS if w <= tiles * P - done)
+                    for g in range(PASSES):
+                        first = g * TOKENS + first_tile * P + done
+                        nc.tensor.matmul_mx(
+                            out=acc_of[bank][:, columns.start + done : columns.start + done + width],
+                            lhsT=w_codes[:, g * P : (g + 1) * P].bitcast(FP8X4),
+                            lhsT_scale=w_scales[:, g * P : (g + 1) * P],
+                            rhs=h_codes[:, first : first + width].bitcast(FP8X4),
+                            rhs_scale=h_scales[:, first : first + width],
+                            start=(g == 0),
+                            stop=(g == PASSES - 1),
+                        )
+                    done += width
 
         def bias_gain_square(bank):
             s, h, heads = BANKS[bank]
             acc = acc_of[bank]
-            scaled = stage.tile([P, TOKENS], F32, name="scaled")
-            for head, columns, token in pieces(bank):
+            width = heads * SECTIONS[s][2] * P
+            scaled = stage.tile([P, width], F32, name="scaled")
+            for head, columns in pieces(bank):
                 nc.scalar.activation(
                     out=scaled[:, columns],
                     in_=acc[:, columns],
@@ -244,12 +247,12 @@ def tile_dynamicselfattention_pa_kernel(
                     scale=gain_col[:, head : head + 1],
                 )
             scaled_of[bank] = scaled
-            if h == 0:
-                square = const.tile([P, TOKENS], F32, name="square_sum_%d" % s)
+            if h == 0 and s < LAST:
+                square = const.tile([P, width], F32, name="square_sum_%d" % s)
                 square_sum[s] = square
             else:
-                square = stage.tile([P, TOKENS], F32, name="square")
-            for head, columns, token in pieces(bank):
+                square = stage.tile([P, width], F32, name="square")
+            for head, columns in pieces(bank):
                 nc.scalar.activation(
                     out=square[:, columns],
                     in_=acc[:, columns],
@@ -257,7 +260,9 @@ def tile_dynamicselfattention_pa_kernel(
                     bias=bias_col[:, head : head + 1],
                     scale=1.0,
                 )
-            if bank == last_bank_of[s]:
+            if s == LAST:
+                square_of[bank] = square
+            elif bank == last_bank_of[s]:
                 last_square[s] = square
             elif h > 0:
                 nc.gpsimd.tensor_tensor(
@@ -266,7 +271,8 @@ def tile_dynamicselfattention_pa_kernel(
 
         def turn_back(bank):
             back = back_pool.tile([P, TOKEN_TILES, HEAD_DIM], F32, name="back")
-            for j in range(TOKEN_TILES):
+            s, h, heads = BANKS[bank]
+            for j in range(heads * SECTIONS[s][2]):
                 nc.tensor.transpose(
                     back[:, j, :], scaled_of[bank][:, j * P : (j + 1) * P], ident[:]
                 )
@@ -277,7 +283,7 @@ def tile_dynamicselfattention_pa_kernel(
             half, first_tile, tiles = SECTIONS[s]
             if h == 0:
                 rotated[s] = const.tile([P, tiles, HEADS, HEAD_DIM], F32, name="rotated_%d" % s)
-            x = back[:].rearrange("p (i t) d -> p i t d", i=heads)
+            x = back[:, 0 : heads * tiles, :].rearrange("p (i t) d -> p i t d", i=heads)
             low, high = slice(0, HALF_DIM), slice(HALF_DIM, HEAD_DIM)
             shape = [P, heads, tiles, HEAD_DIM]
             half_shape = [P, heads, tiles, HALF_DIM]
@@ -297,6 +303,11 @@ def tile_dynamicselfattention_pa_kernel(
                     in1=sin_signed[:, these, to].unsqueeze(1).to_broadcast(half_shape),
                     op=ALU.mult,
                 )
+            products_of[bank] = (straight, crossed)
+
+        def add_products(bank):
+            s, h, heads = BANKS[bank]
+            straight, crossed = products_of[bank]
             nc.vector.tensor_tensor(
                 out=rotated[s][:, :, h : h + heads, :].rearrange("p t i d -> p i t d"),
                 in0=straight[:],
@@ -304,10 +315,11 @@ def tile_dynamicselfattention_pa_kernel(
                 op=ALU.add,
             )
 
-        def inverse_rms(s):
+        def turn_squares(s):
             half, first_tile, tiles = SECTIONS[s]
+            heads = BANKS[last_bank_of[s]][2]
             sums_back = back_pool.tile([P, TOKEN_TILES, HEAD_DIM], F32, name="back")
-            for j in range(TOKEN_TILES):
+            for j in range(heads * tiles):
                 for squares, first in ((square_sum[s], True), (last_square[s], False)):
                     nc.tensor.matmul(
                         out=sums_back[:, j, :],
@@ -317,12 +329,29 @@ def tile_dynamicselfattention_pa_kernel(
                         start=first,
                         stop=not first,
                     )
+            return sums_back[:, 0 : heads * tiles, :]
+
+        def turn_squares_of_bank(bank, last_sums):
+            s, h, heads = BANKS[bank]
+            for i in range(heads):
+                nc.tensor.matmul(
+                    out=last_sums[:, 0, 0, :],
+                    lhsT=square_of[bank][:, i * P : (i + 1) * P],
+                    rhs=ident[:],
+                    is_transpose=True,
+                    start=(h + i == 0),
+                    stop=(h + i == HEADS - 1),
+                )
+
+        def root_mean_square(s, sums_back):
+            half, first_tile, tiles = SECTIONS[s]
+            heads = BANKS[last_bank_of[s]][2] if s < LAST else 1
             total = const.tile([P, tiles], F32, name="total_%d" % s)
-            by_tile = sums_back[:].rearrange("p (i t) d -> p t i d", t=tiles)
-            unused = stage.tile([P, TOKEN_TILES // tiles, HEAD_DIM], F32, name="unused")
+            by_tile = sums_back.rearrange("p (i t) d -> p t i d", t=tiles)
+            unused = stage.tile([P, tiles, heads, HEAD_DIM], F32, name="unused")
             for t in range(tiles):
                 nc.scalar.activation(
-                    out=unused[:],
+                    out=unused[:, t, :, :],
                     in_=by_tile[:, t, :, :],
                     func=ACT.Copy,
                     accum_out=total[:, t : t + 1],
@@ -332,17 +361,21 @@ def tile_dynamicselfattention_pa_kernel(
                 out=rms[:], in_=total[:], func=ACT.Sqrt, bias=eps_col[:, 0:1], scale=1.0 / DIM
             )
             inv_rms = const.tile([P, tiles], F32, name="inv_rms_%d" % s)
-            nc.vector.reciprocal(out=inv_rms[:], in_=rms[:])
             inv_rms_of[s] = inv_rms
+            rms_of[s] = rms
 
-        def scale_and_store(s, t, side):
+        def scale_and_store(s, t, part, engine):
             half, first_tile, tiles = SECTIONS[s]
-            heads = slice(side * HEADS // 2, (side + 1) * HEADS // 2)
-            columns = slice(side * DIM // 2, (side + 1) * DIM // 2)
+            heads = slice(part * HEADS // PARTS, (part + 1) * HEADS // PARTS)
+            columns = slice(part * DIM // PARTS, (part + 1) * DIM // PARTS)
             row = rotated[s][:, t, heads, :].rearrange("p h d -> p (h d)")
             factor = inv_rms_of[s][:, t : t + 1]
-            if s == 1:
+            if engine == "scalar":
                 nc.scalar.activation(out=row, in_=row, func=ACT.Copy, scale=factor)
+            elif engine == "gpsimd":
+                nc.gpsimd.tensor_scalar(
+                    out=row, in0=row, scalar1=factor, scalar2=0.0, op0=ALU.mult, op1=ALU.add
+                )
             else:
                 nc.vector.tensor_scalar(
                     out=row, in0=row, scalar1=factor, scalar2=None, op0=ALU.mult
@@ -351,50 +384,50 @@ def tile_dynamicselfattention_pa_kernel(
             nc.sync.dma_start(out=outs[half][token : token + P, columns], in_=row)
 
         LEAD = 3
-
-        def heads_ready(step):
-            return max(0, min(ALL_HEADS, (4 * (step + 1) + 2) // 3))
-
-        def heads_of(step):
-            return range(heads_ready(step - 1), heads_ready(step))
-
         tail = []
-        for step in range(len(BANKS) + LEAD + 3):
-            for head in heads_of(step):
-                if head + PREFETCH < ALL_HEADS:
-                    load_weights(head + PREFETCH)
-            for head in heads_of(step - 1):
-                regroup_weights(head)
-            for head in heads_of(step - 2):
-                quantise(head)
+        for step in range(len(BANKS) + LEAD + 2):
             bank = step - LEAD
             turned = bank - 2
+            done = [s for s in last_bank_of if last_bank_of[s] == turned]
+            if step + PREFETCH < ALL_HEADS:
+                load_weights(step + PREFETCH)
             if 0 <= turned < len(BANKS):
                 back = turn_back(turned)
-            fresh = heads_of(step)
             if 0 <= bank < len(BANKS):
-                parts = max(1, len(fresh))
-                for part in range(parts):
-                    multiply(bank, part, parts)
-                    if part < len(fresh):
-                        flip(fresh[part])
-            else:
-                for head in fresh:
-                    flip(head)
+                multiply(bank)
+            if 0 <= turned < len(BANKS) and BANKS[turned][0] == LAST:
+                if BANKS[turned][1] == 0:
+                    last_sums = flipped_pool.tile([P, 2, 2, P], F32, name="flipped")
+                turn_squares_of_bank(turned, last_sums)
+            for s in done:
+                sums_back = turn_squares(s) if s < LAST else last_sums[:, 0, 0:1, :]
+            if step < ALL_HEADS:
+                flip(step)
+            if 0 <= step - 1 < ALL_HEADS:
+                regroup_weights(step - 1)
             if 0 <= bank - 1 < len(BANKS):
                 bias_gain_square(bank - 1)
+            for s in done:
+                root_mean_square(s, sums_back)
             if 0 <= turned < len(BANKS):
                 rotate(turned, back)
-            if tail:
-                scale_and_store(*tail.pop(0))
-            for s, (half, first_tile, tiles) in enumerate(SECTIONS):
-                settle = 0 if s == len(SECTIONS) - 1 else 1
-                if turned == last_bank_of[s] + settle:
-                    inverse_rms(s)
-                    tail.extend((s, t, side) for t in range(tiles) for side in range(2))
+            if 0 <= step - 2 < ALL_HEADS:
+                quantise(step - 2)
+            if 0 <= turned < len(BANKS):
+                add_products(turned)
+            for s in done:
+                nc.vector.reciprocal(out=inv_rms_of[s][:], in_=rms_of[s][:])
+            for piece in range(1 if step < ALL_HEADS + LEAD + 2 else 4):
+                if tail:
+                    scale_and_store(*tail.pop(0))
+            for s in done:
+                engines = ["scalar", "gpsimd"] if 0 < s < LAST else ["vector"]
+                pieces_of_s = [(t, part) for t in range(SECTIONS[s][2]) for part in range(PARTS)]
+                for i, (t, part) in enumerate(pieces_of_s):
+                    tail.append((s, t, part, engines[i % len(engines)]))
             if step == 2:
                 make_bias_and_gain()
             if step == 3:
                 make_rope_tables()
-        for args in tail:
-            scale_and_store(*args)
+        for piece in tail:
+            scale_and_store(*piece)

@@ -25,6 +25,7 @@ PAIRS = PASSES // 2
 WORDS = K_PASS // 2
 PREFETCH = 6
 PARTS = 4
+BRIDGE = 32
 EPS = 1e-6
 
 FLOPS = 2 * TOKENS * 2 * DIM * DIM
@@ -84,7 +85,12 @@ def tile_dynamicselfattention_pa_kernel(
         hidden_tiles = []
         for t in range(TOKEN_TILES):
             rows = rows_pool.tile([P, DIM], BF16, name="rows")
-            nc.sync.dma_start(out=rows[:], in_=hidden_rows[t * P : (t + 1) * P, :])
+            width = DIM if 0 < t < TOKEN_TILES - 1 else DIM // 2
+            for first in range(0, DIM, width):
+                nc.sync.dma_start(
+                    out=rows[:, first : first + width],
+                    in_=hidden_rows[t * P : (t + 1) * P, first : first + width],
+                )
             hidden_tiles.append(rows)
         load_weights(0)
         load_weights(1)
@@ -106,6 +112,8 @@ def tile_dynamicselfattention_pa_kernel(
         for head in range(2, PREFETCH):
             load_weights(head)
 
+        zeros = const.tile([P, P], BF16)
+        nc.gpsimd.memset(zeros[:], 0.0)
         ident = const.tile([P, P], F32)
         make_identity(nc, ident[:])
         eps_col = const.tile([P, 1], F32)
@@ -113,8 +121,13 @@ def tile_dynamicselfattention_pa_kernel(
         warm = const.tile([P, 1], F32)
         nc.scalar.activation(out=warm[:], in_=eps_col[:], func=ACT.Sqrt)
 
-        def transpose_words(rows_words, pair):
+        def bridge(out):
+            nc.tensor.matmul(out=out, lhsT=zeros[:], rhs=zeros[:, 0:BRIDGE], start=True, stop=True)
+
+        def transpose_words(rows_words, pair, after_mx=False):
             flipped = flipped_pool.tile([P, 2, 2, P], F32, name="flipped")
+            if after_mx:
+                bridge(flipped[:, 0, 0, 0:BRIDGE])
             for g2 in range(2):
                 for u in range(2):
                     first = (2 * pair + g2) * WORDS + u
@@ -140,12 +153,14 @@ def tile_dynamicselfattention_pa_kernel(
                     h_grouped_words[:, 2 * pair : 2 * pair + 2, t * P : (t + 1) * P, :],
                     copy,
                 )
-        for g in range(PASSES):
-            nc.vector.quantize_mx(
-                out=h_codes[:, g * TOKENS : (g + 1) * TOKENS].bitcast(FP8X4),
-                scales=h_scales[:, g * TOKENS : (g + 1) * TOKENS],
-                in_=h_grouped[:, g * TOKENS * 4 : (g + 1) * TOKENS * 4],
-            )
+            if t % 2 == 1:
+                for g in range(PASSES):
+                    columns = slice(g * TOKENS + (t - 1) * P, g * TOKENS + (t + 1) * P)
+                    nc.vector.quantize_mx(
+                        out=h_codes[:, columns].bitcast(FP8X4),
+                        scales=h_scales[:, columns],
+                        in_=h_grouped[:, columns.start * 4 : columns.stop * 4],
+                    )
 
         vec_rows = const.tile([P, P], F32)
         vec_cols = const.tile([P, P], F32)
@@ -179,7 +194,8 @@ def tile_dynamicselfattention_pa_kernel(
 
         def flip(head):
             flipped_of[head] = [
-                transpose_words(weight_rows[head][:].bitcast(F32), pair) for pair in range(PAIRS)
+                transpose_words(weight_rows[head][:].bitcast(F32), pair, after_mx=(pair == 0))
+                for pair in range(PAIRS)
             ]
 
         def regroup_weights(head):
@@ -215,6 +231,7 @@ def tile_dynamicselfattention_pa_kernel(
         def multiply(bank):
             half, first_tile, tiles = SECTIONS[BANKS[bank][0]]
             acc_of[bank] = acc_pool.tile([P, TOKENS], F32, name="acc")
+            bridge(acc_of[bank][:, 0:BRIDGE])
             for head, columns in pieces(bank):
                 w_codes, w_scales = codes_of[head]
                 done = 0

@@ -23,9 +23,8 @@ K_PASS = 4 * P
 PASSES = DIM // K_PASS
 PAIRS = PASSES // 2
 WORDS = K_PASS // 2
-PREFETCH = 6
+PREFETCH = 5
 PARTS = 4
-BRIDGE = 32
 EPS = 1e-6
 
 FLOPS = 2 * TOKENS * 2 * DIM * DIM
@@ -52,6 +51,7 @@ def tile_dynamicselfattention_pa_kernel(
         const = ctx.enter_context(tc.tile_pool(name="const", bufs=1))
         rows_pool = ctx.enter_context(tc.tile_pool(name="rows", bufs=TOKEN_TILES + PREFETCH))
         stage = ctx.enter_context(tc.tile_pool(name="stage", bufs=3))
+        late_pool = ctx.enter_context(tc.tile_pool(name="late", bufs=4))
         q_codes_pool = ctx.enter_context(tc.tile_pool(name="q_codes", bufs=3))
         k_codes_pool = ctx.enter_context(tc.tile_pool(name="k_codes", bufs=HEADS))
         flipped_pool = ctx.enter_context(tc.psum_pool(name="flipped", bufs=4))
@@ -71,6 +71,7 @@ def tile_dynamicselfattention_pa_kernel(
         LAST = len(SECTIONS) - 1
         last_bank_of = {s: max(b for b in range(len(BANKS)) if BANKS[b][0] == s) for s in range(len(SECTIONS))}
         products_of = {}
+        back_of = {}
         rotated = {}
         inv_rms_of = {}
         rms_of = {}
@@ -94,6 +95,8 @@ def tile_dynamicselfattention_pa_kernel(
             hidden_tiles.append(rows)
         load_weights(0)
         load_weights(1)
+        load_weights(2)
+        load_weights(3)
         nc.sync.dma_start(
             out=vec_rows_bf[0:ALL_HEADS, :], in_=b_qk.rearrange("(h d) -> h d", d=HEAD_DIM)
         )
@@ -109,11 +112,9 @@ def tile_dynamicselfattention_pa_kernel(
         nc.sync.dma_start(out=cos_bf[:], in_=cos.rearrange("(t p) d -> p t d", p=P))
         sin_bf = const.tile([P, TOKEN_TILES, HEAD_DIM], BF16)
         nc.sync.dma_start(out=sin_bf[:], in_=sin.rearrange("(t p) d -> p t d", p=P))
-        for head in range(2, PREFETCH):
+        for head in range(4, PREFETCH):
             load_weights(head)
 
-        zeros = const.tile([P, P], BF16)
-        nc.gpsimd.memset(zeros[:], 0.0)
         ident = const.tile([P, P], F32)
         make_identity(nc, ident[:])
         eps_col = const.tile([P, 1], F32)
@@ -121,13 +122,8 @@ def tile_dynamicselfattention_pa_kernel(
         warm = const.tile([P, 1], F32)
         nc.scalar.activation(out=warm[:], in_=eps_col[:], func=ACT.Sqrt)
 
-        def bridge(out):
-            nc.tensor.matmul(out=out, lhsT=zeros[:], rhs=zeros[:, 0:BRIDGE], start=True, stop=True)
-
-        def transpose_words(rows_words, pair, after_mx=False):
+        def transpose_words(rows_words, pair):
             flipped = flipped_pool.tile([P, 2, 2, P], F32, name="flipped")
-            if after_mx:
-                bridge(flipped[:, 0, 0, 0:BRIDGE])
             for g2 in range(2):
                 for u in range(2):
                     first = (2 * pair + g2) * WORDS + u
@@ -194,8 +190,7 @@ def tile_dynamicselfattention_pa_kernel(
 
         def flip(head):
             flipped_of[head] = [
-                transpose_words(weight_rows[head][:].bitcast(F32), pair, after_mx=(pair == 0))
-                for pair in range(PAIRS)
+                transpose_words(weight_rows[head][:].bitcast(F32), pair) for pair in range(PAIRS)
             ]
 
         def regroup_weights(head):
@@ -230,8 +225,11 @@ def tile_dynamicselfattention_pa_kernel(
 
         def multiply(bank):
             half, first_tile, tiles = SECTIONS[BANKS[bank][0]]
-            acc_of[bank] = acc_pool.tile([P, TOKENS], F32, name="acc")
-            bridge(acc_of[bank][:, 0:BRIDGE])
+            if BANKS[bank][0] < LAST:
+                acc_of[bank] = acc_pool.tile([P, TOKENS], F32, name="acc")
+            else:
+                spare = flipped_pool.tile([P, 2, 2, P], F32, name="flipped")
+                acc_of[bank] = spare[:].rearrange("p g u r -> p (g u r)")
             for head, columns in pieces(bank):
                 w_codes, w_scales = codes_of[head]
                 done = 0
@@ -254,21 +252,17 @@ def tile_dynamicselfattention_pa_kernel(
             s, h, heads = BANKS[bank]
             acc = acc_of[bank]
             width = heads * SECTIONS[s][2] * P
-            scaled = stage.tile([P, width], F32, name="scaled")
-            for head, columns in pieces(bank):
-                nc.scalar.activation(
-                    out=scaled[:, columns],
-                    in_=acc[:, columns],
-                    func=ACT.Identity,
-                    bias=gain_bias_col[:, head : head + 1],
-                    scale=gain_col[:, head : head + 1],
-                )
+            pool = late_pool if s == LAST else stage
+            scaled = pool.tile([P, width], F32, name="scaled")
             scaled_of[bank] = scaled
             if h == 0 and s < LAST:
                 square = const.tile([P, width], F32, name="square_sum_%d" % s)
                 square_sum[s] = square
             else:
                 square = stage.tile([P, width], F32, name="square")
+
+            if s < LAST:
+                scale_bank(bank)
             for head, columns in pieces(bank):
                 nc.scalar.activation(
                     out=square[:, columns],
@@ -286,6 +280,17 @@ def tile_dynamicselfattention_pa_kernel(
                     out=square_sum[s][:], in0=square_sum[s][:], in1=square[:], op=ALU.add
                 )
 
+        def scale_bank(bank):
+            acc, scaled = acc_of[bank], scaled_of[bank]
+            for head, columns in pieces(bank):
+                nc.scalar.activation(
+                    out=scaled[:, columns],
+                    in_=acc[:, columns],
+                    func=ACT.Identity,
+                    bias=gain_bias_col[:, head : head + 1],
+                    scale=gain_col[:, head : head + 1],
+                )
+
         def turn_back(bank):
             back = back_pool.tile([P, TOKEN_TILES, HEAD_DIM], F32, name="back")
             s, h, heads = BANKS[bank]
@@ -301,36 +306,54 @@ def tile_dynamicselfattention_pa_kernel(
             if h == 0:
                 rotated[s] = const.tile([P, tiles, HEADS, HEAD_DIM], F32, name="rotated_%d" % s)
             x = back[:, 0 : heads * tiles, :].rearrange("p (i t) d -> p i t d", i=heads)
-            low, high = slice(0, HALF_DIM), slice(HALF_DIM, HEAD_DIM)
             shape = [P, heads, tiles, HEAD_DIM]
-            half_shape = [P, heads, tiles, HALF_DIM]
             these = slice(first_tile, first_tile + tiles)
+            cos_table = cos_f[:, these, :].unsqueeze(1).to_broadcast(shape)
+            sin_table = sin_signed[:, these, :].unsqueeze(1).to_broadcast(shape)
             straight = stage.tile(shape, F32, name="straight")
-            nc.vector.tensor_tensor(
-                out=straight[:],
-                in0=x,
-                in1=cos_f[:, these, :].unsqueeze(1).to_broadcast(shape),
-                op=ALU.mult,
-            )
             crossed = stage.tile(shape, F32, name="crossed")
-            for to, source in ((low, high), (high, low)):
+            if s < LAST:
+                nc.vector.tensor_tensor(out=straight[:], in0=x, in1=cos_table, op=ALU.mult)
+                halves = "p i t (two h) -> p i t two h"
                 nc.vector.tensor_tensor(
-                    out=crossed[:, :, :, to],
-                    in0=x[:, :, :, source],
-                    in1=sin_signed[:, these, to].unsqueeze(1).to_broadcast(half_shape),
+                    out=crossed[:].rearrange(halves, two=2),
+                    in0=x.rearrange(halves, two=2)[:, :, :, ::-1, :],
+                    in1=sin_table.rearrange(halves, two=2),
                     op=ALU.mult,
                 )
+            else:
+                low, high = slice(0, HALF_DIM), slice(HALF_DIM, HEAD_DIM)
+                for out, source, table in (
+                    (straight[:], x, cos_table),
+                    (crossed[:, :, :, low], x[:, :, :, high], sin_table[:, :, :, low]),
+                    (crossed[:, :, :, high], x[:, :, :, low], sin_table[:, :, :, high]),
+                ):
+                    nc.vector.scalar_tensor_tensor(
+                        out=out,
+                        in0=source,
+                        scalar=inv_rms_of[s][:, 0:1],
+                        in1=table,
+                        op0=ALU.mult,
+                        op1=ALU.mult,
+                    )
             products_of[bank] = (straight, crossed)
 
         def add_products(bank):
             s, h, heads = BANKS[bank]
+            half, first_tile, tiles = SECTIONS[s]
             straight, crossed = products_of[bank]
-            nc.vector.tensor_tensor(
+            engine = nc.gpsimd if s == LAST and bank < len(BANKS) - 1 else nc.vector
+            engine.tensor_tensor(
                 out=rotated[s][:, :, h : h + heads, :].rearrange("p t i d -> p i t d"),
                 in0=straight[:],
                 in1=crossed[:],
                 op=ALU.add,
             )
+            if s == LAST:
+                nc.sync.dma_start(
+                    out=outs[half][first_tile * P :, h * HEAD_DIM : (h + heads) * HEAD_DIM],
+                    in_=rotated[s][:, 0, h : h + heads, :].rearrange("p h d -> p (h d)"),
+                )
 
         def turn_squares(s):
             half, first_tile, tiles = SECTIONS[s]
@@ -352,7 +375,7 @@ def tile_dynamicselfattention_pa_kernel(
             s, h, heads = BANKS[bank]
             for i in range(heads):
                 nc.tensor.matmul(
-                    out=last_sums[:, 0, 0, :],
+                    out=last_sums[:, 0:P],
                     lhsT=square_of[bank][:, i * P : (i + 1) * P],
                     rhs=ident[:],
                     is_transpose=True,
@@ -389,10 +412,6 @@ def tile_dynamicselfattention_pa_kernel(
             factor = inv_rms_of[s][:, t : t + 1]
             if engine == "scalar":
                 nc.scalar.activation(out=row, in_=row, func=ACT.Copy, scale=factor)
-            elif engine == "gpsimd":
-                nc.gpsimd.tensor_scalar(
-                    out=row, in0=row, scalar1=factor, scalar2=0.0, op0=ALU.mult, op1=ALU.add
-                )
             else:
                 nc.vector.tensor_scalar(
                     out=row, in0=row, scalar1=factor, scalar2=None, op0=ALU.mult
@@ -401,50 +420,81 @@ def tile_dynamicselfattention_pa_kernel(
             nc.sync.dma_start(out=outs[half][token : token + P, columns], in_=row)
 
         LEAD = 3
+        EARLY = 2
+        late = [b for b in range(len(BANKS)) if BANKS[b][0] == LAST]
+        multiply_at = {b: b + LEAD - (EARLY if b in late else 0) for b in range(len(BANKS))}
+        turn_at = {b: b + LEAD + (3 if b in late else 2) for b in range(len(BANKS))}
+        rotate_at = {b: turn_at[b] + (1 if b in late else 0) for b in range(len(BANKS))}
+        SCALERS = {0: ["vector"], 1: ["vector"] * 8 + ["scalar"] * 4}
         tail = []
-        for step in range(len(BANKS) + LEAD + 2):
-            bank = step - LEAD
-            turned = bank - 2
-            done = [s for s in last_bank_of if last_bank_of[s] == turned]
+        STORES_ONLY = ALL_HEADS + LEAD + 2
+        for step in range(max(rotate_at.values()) + 1):
+            multiplied = [b for b in range(len(BANKS)) if multiply_at[b] == step]
+            squared = [b for b in range(len(BANKS)) if multiply_at[b] + 1 == step]
+            summed = [b for b in late[:-1] if multiply_at[b] + 2 == step]
+            turned = [b for b in range(len(BANKS)) if turn_at[b] == step]
+            rotated_now = [b for b in range(len(BANKS)) if rotate_at[b] == step]
+            done = [
+                s
+                for s in last_bank_of
+                if multiply_at[last_bank_of[s]] + (1 if s == LAST else 2) == step
+            ]
             if step + PREFETCH < ALL_HEADS:
                 load_weights(step + PREFETCH)
-            if 0 <= turned < len(BANKS):
-                back = turn_back(turned)
-            if 0 <= bank < len(BANKS):
-                multiply(bank)
-            if 0 <= turned < len(BANKS) and BANKS[turned][0] == LAST:
-                if BANKS[turned][1] == 0:
-                    last_sums = flipped_pool.tile([P, 2, 2, P], F32, name="flipped")
-                turn_squares_of_bank(turned, last_sums)
-            for s in done:
-                sums_back = turn_squares(s) if s < LAST else last_sums[:, 0, 0:1, :]
+            for b in turned:
+                if b not in late:
+                    back_of[b] = turn_back(b)
+            sums = {}
+            if step >= ALL_HEADS:
+                sums = {s: turn_squares(s) for s in done if s < LAST}
+            for b in multiplied:
+                multiply(b)
+            if step < ALL_HEADS:
+                sums = {s: turn_squares(s) for s in done if s < LAST}
+            for b in summed:
+                if b == late[0]:
+                    last_sums = acc_pool.tile([P, TOKENS], F32, name="acc")
+                turn_squares_of_bank(b, last_sums)
+            for b in turned:
+                if b in late:
+                    back_of[b] = turn_back(b)
             if step < ALL_HEADS:
                 flip(step)
             if 0 <= step - 1 < ALL_HEADS:
                 regroup_weights(step - 1)
-            if 0 <= bank - 1 < len(BANKS):
-                bias_gain_square(bank - 1)
+            for b in squared:
+                bias_gain_square(b)
+            if LAST in done:
+                turn_squares_of_bank(late[-1], last_sums)
+                sums[LAST] = last_sums[:, 0:P].unsqueeze(1)
             for s in done:
-                root_mean_square(s, sums_back)
-            if 0 <= turned < len(BANKS):
-                rotate(turned, back)
+                root_mean_square(s, sums[s])
+            for b in squared:
+                if b in late:
+                    scale_bank(b)
+            if step >= STORES_ONLY:
+                now, tail = tail[:8], tail[8:]
+                for piece in now:
+                    scale_and_store(*piece)
+            if LAST in done:
+                nc.vector.reciprocal(out=inv_rms_of[LAST][:], in_=rms_of[LAST][:])
+            for b in rotated_now:
+                rotate(b, back_of[b])
             if 0 <= step - 2 < ALL_HEADS:
                 quantise(step - 2)
-            if 0 <= turned < len(BANKS):
-                add_products(turned)
+            for b in rotated_now:
+                add_products(b)
             for s in done:
-                nc.vector.reciprocal(out=inv_rms_of[s][:], in_=rms_of[s][:])
-            for piece in range(1 if step < ALL_HEADS + LEAD + 2 else 4):
-                if tail:
-                    scale_and_store(*tail.pop(0))
+                if s < LAST:
+                    nc.vector.reciprocal(out=inv_rms_of[s][:], in_=rms_of[s][:])
+            if step < STORES_ONLY and tail:
+                scale_and_store(*tail.pop(0))
             for s in done:
-                engines = ["scalar", "gpsimd"] if 0 < s < LAST else ["vector"]
-                pieces_of_s = [(t, part) for t in range(SECTIONS[s][2]) for part in range(PARTS)]
-                for i, (t, part) in enumerate(pieces_of_s):
-                    tail.append((s, t, part, engines[i % len(engines)]))
-            if step == 2:
-                make_bias_and_gain()
+                if s < LAST:
+                    order = [(t, part) for t in range(SECTIONS[s][2]) for part in range(PARTS)]
+                    for i, (t, part) in enumerate(order):
+                        tail.append((s, t, part, SCALERS[s][i % len(SCALERS[s])]))
             if step == 3:
+                make_bias_and_gain()
+            if step == 4:
                 make_rope_tables()
-        for piece in tail:
-            scale_and_store(*piece)

@@ -24,7 +24,7 @@ PASSES = DIM // K_PASS
 PAIRS = PASSES // 2
 WORDS = K_PASS // 2
 PREFETCH = 5
-PARTS = 4
+PARTS = 2
 EPS = 1e-6
 
 FLOPS = 2 * TOKENS * 2 * DIM * DIM
@@ -273,8 +273,8 @@ def tile_dynamicselfattention_pa_kernel(
                 )
             if s == LAST:
                 square_of[bank] = square
-            elif bank == last_bank_of[s]:
-                last_square[s] = square
+            elif bank > last_bank_of[s] - 1:
+                last_square.setdefault(s, []).append(square)
             elif h > 0:
                 nc.gpsimd.tensor_tensor(
                     out=square_sum[s][:], in0=square_sum[s][:], in1=square[:], op=ALU.add
@@ -360,14 +360,15 @@ def tile_dynamicselfattention_pa_kernel(
             heads = BANKS[last_bank_of[s]][2]
             sums_back = back_pool.tile([P, TOKEN_TILES, HEAD_DIM], F32, name="back")
             for j in range(heads * tiles):
-                for squares, first in ((square_sum[s], True), (last_square[s], False)):
+                terms = [square_sum[s]] + last_square[s]
+                for i, squares in enumerate(terms):
                     nc.tensor.matmul(
                         out=sums_back[:, j, :],
                         lhsT=squares[:, j * P : (j + 1) * P],
                         rhs=ident[:],
                         is_transpose=True,
-                        start=first,
-                        stop=not first,
+                        start=(i == 0),
+                        stop=(i == len(terms) - 1),
                     )
             return sums_back[:, 0 : heads * tiles, :]
 
@@ -425,9 +426,9 @@ def tile_dynamicselfattention_pa_kernel(
         multiply_at = {b: b + LEAD - (EARLY if b in late else 0) for b in range(len(BANKS))}
         turn_at = {b: b + LEAD + (3 if b in late else 2) for b in range(len(BANKS))}
         rotate_at = {b: turn_at[b] + (1 if b in late else 0) for b in range(len(BANKS))}
-        SCALERS = {0: ["vector"], 1: ["vector"] * 8 + ["scalar"] * 4}
+        SCALERS = {0: ["vector"], 1: ["vector"] * 3 + ["scalar"] * 3}
         tail = []
-        STORES_ONLY = ALL_HEADS + LEAD + 2
+        STORES_ONLY = 36
         for step in range(max(rotate_at.values()) + 1):
             multiplied = [b for b in range(len(BANKS)) if multiply_at[b] == step]
             squared = [b for b in range(len(BANKS)) if multiply_at[b] + 1 == step]
@@ -437,43 +438,39 @@ def tile_dynamicselfattention_pa_kernel(
             done = [
                 s
                 for s in last_bank_of
-                if multiply_at[last_bank_of[s]] + (1 if s == LAST else 2) == step
+                if multiply_at[last_bank_of[s]] + (2 if s == 0 else 1) == step
             ]
             if step + PREFETCH < ALL_HEADS:
                 load_weights(step + PREFETCH)
             for b in turned:
                 if b not in late:
                     back_of[b] = turn_back(b)
-            sums = {}
-            if step >= ALL_HEADS:
-                sums = {s: turn_squares(s) for s in done if s < LAST}
+            if 0 <= step - 1 < ALL_HEADS:
+                regroup_weights(step - 1)
+            for b in squared:
+                bias_gain_square(b)
+            sums = {s: turn_squares(s) for s in done if s < LAST}
             for b in multiplied:
                 multiply(b)
-            if step < ALL_HEADS:
-                sums = {s: turn_squares(s) for s in done if s < LAST}
             for b in summed:
                 if b == late[0]:
                     last_sums = acc_pool.tile([P, TOKENS], F32, name="acc")
                 turn_squares_of_bank(b, last_sums)
+            if LAST in done:
+                turn_squares_of_bank(late[-1], last_sums)
+                sums[LAST] = last_sums[:, 0:P].unsqueeze(1)
             for b in turned:
                 if b in late:
                     back_of[b] = turn_back(b)
             if step < ALL_HEADS:
                 flip(step)
-            if 0 <= step - 1 < ALL_HEADS:
-                regroup_weights(step - 1)
-            for b in squared:
-                bias_gain_square(b)
-            if LAST in done:
-                turn_squares_of_bank(late[-1], last_sums)
-                sums[LAST] = last_sums[:, 0:P].unsqueeze(1)
             for s in done:
                 root_mean_square(s, sums[s])
             for b in squared:
                 if b in late:
                     scale_bank(b)
             if step >= STORES_ONLY:
-                now, tail = tail[:8], tail[8:]
+                now, tail = tail[:3], tail[3:]
                 for piece in now:
                     scale_and_store(*piece)
             if LAST in done:
@@ -487,11 +484,11 @@ def tile_dynamicselfattention_pa_kernel(
             for s in done:
                 if s < LAST:
                     nc.vector.reciprocal(out=inv_rms_of[s][:], in_=rms_of[s][:])
-            if step < STORES_ONLY and tail:
+            if step < STORES_ONLY and tail and step % 2 == 0:
                 scale_and_store(*tail.pop(0))
             for s in done:
                 if s < LAST:
-                    order = [(t, part) for t in range(SECTIONS[s][2]) for part in range(PARTS)]
+                    order = [(t, part) for part in range(PARTS) for t in range(SECTIONS[s][2])]
                     for i, (t, part) in enumerate(order):
                         tail.append((s, t, part, SCALERS[s][i % len(SCALERS[s])]))
             if step == 3:

@@ -25,6 +25,7 @@ PAIRS = PASSES // 2
 WORDS = K_PASS // 2
 PREFETCH = 5
 PARTS = 2
+WARM_UP = 4
 EPS = 1e-6
 
 FLOPS = 2 * TOKENS * 2 * DIM * DIM
@@ -115,12 +116,22 @@ def tile_dynamicselfattention_pa_kernel(
         for head in range(4, PREFETCH):
             load_weights(head)
 
+        zeros = const.tile([P, TOKENS], BF16)
+        nc.vector.memset(zeros[:], 0.0)
         ident = const.tile([P, P], F32)
         make_identity(nc, ident[:])
         eps_col = const.tile([P, 1], F32)
         nc.vector.memset(eps_col[:], EPS)
         warm = const.tile([P, 1], F32)
         nc.scalar.activation(out=warm[:], in_=eps_col[:], func=ACT.Sqrt)
+
+        warm_out = acc_pool.tile([P, TOKENS], F32, name="acc")
+
+        def keep_warm():
+            nc.tensor.matmul(out=warm_out[:], lhsT=zeros[:, 0:P], rhs=zeros[:], start=True, stop=True)
+
+        for i in range(WARM_UP):
+            keep_warm()
 
         def transpose_words(rows_words, pair):
             flipped = flipped_pool.tile([P, 2, 2, P], F32, name="flipped")
@@ -149,6 +160,7 @@ def tile_dynamicselfattention_pa_kernel(
                     h_grouped_words[:, 2 * pair : 2 * pair + 2, t * P : (t + 1) * P, :],
                     copy,
                 )
+            keep_warm()
             if t % 2 == 1:
                 for g in range(PASSES):
                     columns = slice(g * TOKENS + (t - 1) * P, g * TOKENS + (t + 1) * P)
@@ -464,6 +476,8 @@ def tile_dynamicselfattention_pa_kernel(
                     back_of[b] = turn_back(b)
             if step < ALL_HEADS:
                 flip(step)
+            if step < LEAD:
+                keep_warm()
             for s in done:
                 root_mean_square(s, sums[s])
             for b in squared:

from contextlib import ExitStack

import concourse.mybir as mybir
from concourse.masks import make_identity

F32 = mybir.dt.float32
BF16 = mybir.dt.bfloat16
U32 = mybir.dt.uint32
U8 = mybir.dt.uint8
FP8X4 = mybir.dt.float8_e4m3fn_x4
ACT = mybir.ActivationFunctionType
ALU = mybir.AluOpType

P = 128
TOKENS = 512
TOKEN_TILES = TOKENS // P
DIM = 2048
HEAD_DIM = 128
HALF_DIM = HEAD_DIM // 2
HEADS = DIM // HEAD_DIM
ALL_HEADS = 2 * HEADS
K_PASS = 4 * P
PASSES = DIM // K_PASS
PAIRS = PASSES // 2
WORDS = K_PASS // 2
PREFETCH = 5
PARTS = 2
WARM_UP = 4
EPS = 1e-6

FLOPS = 2 * TOKENS * 2 * DIM * DIM

SECTIONS = [(0, 0, 4), (1, 0, 3), (1, 3, 1)]
BANKS = [
    (s, h, heads)
    for s, heads in enumerate((1, 1, 4))
    for h in range(0, HEADS, heads)
]
MX_WIDTHS = (512, 256, 128)

def tile_dynamicselfattention_pa_kernel(
    tc, hidden_states, cos, sin, w_qk, b_qk, g_q, g_k, out_0, out_1
):
    nc = tc.nc
    hidden_rows = hidden_states.flatten_outer_dims()
    outs = [
        out_0.rearrange("b s h d -> (b s) (h d)"),
        out_1.rearrange("b s h d -> (b s) (h d)"),
    ]

    with ExitStack() as ctx:
        const = ctx.enter_context(tc.tile_pool(name="const", bufs=1))
        rows_pool = ctx.enter_context(tc.tile_pool(name="rows", bufs=TOKEN_TILES + PREFETCH))
        stage = ctx.enter_context(tc.tile_pool(name="stage", bufs=3))
        late_pool = ctx.enter_context(tc.tile_pool(name="late", bufs=4))
        q_codes_pool = ctx.enter_context(tc.tile_pool(name="q_codes", bufs=3))
        k_codes_pool = ctx.enter_context(tc.tile_pool(name="k_codes", bufs=HEADS))
        flipped_pool = ctx.enter_context(tc.psum_pool(name="flipped", bufs=4))
        acc_pool = ctx.enter_context(tc.psum_pool(name="acc", bufs=2))
        back_pool = ctx.enter_context(tc.psum_pool(name="back", bufs=2))
        ctx.enter_context(tc.manual_schedule())

        weight_rows = {}
        flipped_of = {}
        grouped_of = {}
        codes_of = {}
        acc_of = {}
        scaled_of = {}
        square_sum = {}
        last_square = {}
        square_of = {}
        LAST = len(SECTIONS) - 1
        last_bank_of = {s: max(b for b in range(len(BANKS)) if BANKS[b][0] == s) for s in range(len(SECTIONS))}
        products_of = {}
        back_of = {}
        rotated = {}
        inv_rms_of = {}
        rms_of = {}

        def load_weights(head):
            rows = rows_pool.tile([P, DIM], BF16, name="rows")
            nc.sync.dma_start(out=rows[:], in_=w_qk[head * P : (head + 1) * P, :])
            weight_rows[head] = rows

        vec_rows_bf = const.tile([P, P], BF16)
        nc.vector.memset(vec_rows_bf[:], 0.0)
        hidden_tiles = []
        for t in range(TOKEN_TILES):
            rows = rows_pool.tile([P, DIM], BF16, name="rows")
            width = DIM if 0 < t < TOKEN_TILES - 1 else DIM // 2
            for first in range(0, DIM, width):
                nc.sync.dma_start(
                    out=rows[:, first : first + width],
                    in_=hidden_rows[t * P : (t + 1) * P, first : first + width],
                )
            hidden_tiles.append(rows)
        load_weights(0)
        load_weights(1)
        load_weights(2)
        load_weights(3)
        nc.sync.dma_start(
            out=vec_rows_bf[0:ALL_HEADS, :], in_=b_qk.rearrange("(h d) -> h d", d=HEAD_DIM)
        )
        nc.sync.dma_start(
            out=vec_rows_bf[ALL_HEADS : ALL_HEADS + HEADS, :],
            in_=g_q.rearrange("(h d) -> h d", d=HEAD_DIM),
        )
        nc.sync.dma_start(
            out=vec_rows_bf[ALL_HEADS + HEADS : 2 * ALL_HEADS, :],
            in_=g_k.rearrange("(h d) -> h d", d=HEAD_DIM),
        )
        cos_bf = const.tile([P, TOKEN_TILES, HEAD_DIM], BF16)
        nc.sync.dma_start(out=cos_bf[:], in_=cos.rearrange("(t p) d -> p t d", p=P))
        sin_bf = const.tile([P, TOKEN_TILES, HEAD_DIM], BF16)
        nc.sync.dma_start(out=sin_bf[:], in_=sin.rearrange("(t p) d -> p t d", p=P))
        for head in range(4, PREFETCH):
            load_weights(head)

        zeros = const.tile([P, TOKENS], BF16)
        nc.vector.memset(zeros[:], 0.0)
        ident = const.tile([P, P], F32)
        make_identity(nc, ident[:])
        eps_col = const.tile([P, 1], F32)
        nc.vector.memset(eps_col[:], EPS)
        warm = const.tile([P, 1], F32)
        nc.scalar.activation(out=warm[:], in_=eps_col[:], func=ACT.Sqrt)

        warm_out = acc_pool.tile([P, TOKENS], F32, name="acc")

        def keep_warm():
            nc.tensor.matmul(out=warm_out[:], lhsT=zeros[:, 0:P], rhs=zeros[:], start=True, stop=True)

        for i in range(WARM_UP):
            keep_warm()

        def transpose_words(rows_words, pair):
            flipped = flipped_pool.tile([P, 2, 2, P], F32, name="flipped")
            for g2 in range(2):
                for u in range(2):
                    first = (2 * pair + g2) * WORDS + u
                    nc.tensor.transpose(
                        flipped[:, g2, u, :], rows_words[:, first : first + WORDS - u : 2], ident[:]
                    )
            return flipped

        def regroup(flipped, grouped_words, copy):
            copy(out=grouped_words, in_=flipped[:].rearrange("p g u r -> p g r u"))

        h_grouped = const.tile([P, PASSES * TOKENS * 4], BF16, align_bytes=64)
        h_grouped_words = (
            h_grouped[:].bitcast(F32).rearrange("p (g s u) -> p g s u", g=PASSES, u=2)
        )
        h_codes = const.tile([P, PASSES * TOKENS], U32, align_bytes=64)
        h_scales = const.tile([P, PASSES * TOKENS], U8, align_bytes=64)
        for t in range(TOKEN_TILES):
            for pair, copy in enumerate([nc.scalar.copy, nc.vector.tensor_copy]):
                flipped = transpose_words(hidden_tiles[t][:].bitcast(F32), pair)
                regroup(
                    flipped,
                    h_grouped_words[:, 2 * pair : 2 * pair + 2, t * P : (t + 1) * P, :],
                    copy,
                )
            keep_warm()
            if t % 2 == 1:
                for g in range(PASSES):
                    columns = slice(g * TOKENS + (t - 1) * P, g * TOKENS + (t + 1) * P)
                    nc.vector.quantize_mx(
                        out=h_codes[:, columns].bitcast(FP8X4),
                        scales=h_scales[:, columns],
                        in_=h_grouped[:, columns.start * 4 : columns.stop * 4],
                    )

        vec_rows = const.tile([P, P], F32)
        vec_cols = const.tile([P, P], F32)
        bias_col = vec_cols[:, 0:ALL_HEADS]
        gain_col = vec_cols[:, ALL_HEADS : 2 * ALL_HEADS]
        gain_bias_col = const.tile([P, ALL_HEADS], F32)
        cos_f = const.tile([P, TOKEN_TILES, HEAD_DIM], F32)
        sin_signed = const.tile([P, TOKEN_TILES, HEAD_DIM], F32)

        def make_bias_and_gain():
            nc.vector.tensor_copy(out=vec_rows[:], in_=vec_rows_bf[:])
            vec_cols_ps = back_pool.tile([P, TOKEN_TILES, HEAD_DIM], F32, name="back")
            nc.tensor.transpose(vec_cols_ps[:, 0, :], vec_rows[:], ident[:])
            nc.vector.tensor_copy(out=vec_cols[:], in_=vec_cols_ps[:, 0, :])
            nc.vector.tensor_tensor(
                out=gain_bias_col[:], in0=bias_col, in1=gain_col, op=ALU.mult
            )

        def make_rope_tables():
            nc.vector.tensor_copy(out=cos_f[:], in_=cos_bf[:])
            nc.vector.tensor_scalar(
                out=sin_signed[:, :, 0:HALF_DIM],
                in0=sin_bf[:, :, 0:HALF_DIM],
                scalar1=-1.0,
                scalar2=None,
                op0=ALU.mult,
            )
            nc.vector.tensor_copy(
                out=sin_signed[:, :, HALF_DIM:HEAD_DIM], in_=sin_bf[:, :, HALF_DIM:HEAD_DIM]
            )

        def flip(head):
            flipped_of[head] = [
                transpose_words(weight_rows[head][:].bitcast(F32), pair) for pair in range(PAIRS)
            ]

        def regroup_weights(head):
            w_grouped = stage.tile([P, PASSES * P * 4], BF16, name="w_grouped", align_bytes=64)
            w_grouped_words = (
                w_grouped[:].bitcast(F32).rearrange("p (g c u) -> p g c u", g=PASSES, u=2)
            )
            for pair in range(PAIRS):
                regroup(
                    flipped_of[head][pair],
                    w_grouped_words[:, 2 * pair : 2 * pair + 2, :, :],
                    nc.scalar.copy,
                )
            grouped_of[head] = w_grouped

        def quantise(head):
            pool = q_codes_pool if head < HEADS else k_codes_pool
            w_codes = pool.tile([P, PASSES * P], U32, name="w_codes", align_bytes=64)
            w_scales = pool.tile([P, PASSES * P], U8, name="w_scales", align_bytes=64)
            nc.vector.quantize_mx(
                out=w_codes[:].bitcast(FP8X4), scales=w_scales[:], in_=grouped_of[head][:]
            )
            codes_of[head] = (w_codes, w_scales)

        def pieces(bank):
            s, h, heads = BANKS[bank]
            half, first_tile, tiles = SECTIONS[s]
            width = tiles * P
            return [
                (half * HEADS + h + i, slice(i * width, (i + 1) * width)) for i in range(heads)
            ]

        def multiply(bank):
            half, first_tile, tiles = SECTIONS[BANKS[bank][0]]
            if BANKS[bank][0] < LAST:
                acc_of[bank] = acc_pool.tile([P, TOKENS], F32, name="acc")
            else:
                spare = flipped_pool.tile([P, 2, 2, P], F32, name="flipped")
                acc_of[bank] = spare[:].rearrange("p g u r -> p (g u r)")
            for head, columns in pieces(bank):
                w_codes, w_scales = codes_of[head]
                done = 0
                while done < tiles * P:
                    width = max(w for w in MX_WIDTHS if w <= tiles * P - done)
                    for g in range(PASSES):
                        first = g * TOKENS + first_tile * P + done
                        nc.tensor.matmul_mx(
                            out=acc_of[bank][:, columns.start + done : columns.start + done + width],
                            lhsT=w_codes[:, g * P : (g + 1) * P].bitcast(FP8X4),
                            lhsT_scale=w_scales[:, g * P : (g + 1) * P],
                            rhs=h_codes[:, first : first + width].bitcast(FP8X4),
                            rhs_scale=h_scales[:, first : first + width],
                            start=(g == 0),
                            stop=(g == PASSES - 1),
                        )
                    done += width

        def bias_gain_square(bank):
            s, h, heads = BANKS[bank]
            acc = acc_of[bank]
            width = heads * SECTIONS[s][2] * P
            pool = late_pool if s == LAST else stage
            scaled = pool.tile([P, width], F32, name="scaled")
            scaled_of[bank] = scaled
            if h == 0 and s < LAST:
                square = const.tile([P, width], F32, name="square_sum_%d" % s)
                square_sum[s] = square
            else:
                square = stage.tile([P, width], F32, name="square")

            if s < LAST:
                scale_bank(bank)
            for head, columns in pieces(bank):
                nc.scalar.activation(
                    out=square[:, columns],
                    in_=acc[:, columns],
                    func=ACT.Square,
                    bias=bias_col[:, head : head + 1],
                    scale=1.0,
                )
            if s == LAST:
                square_of[bank] = square
            elif bank > last_bank_of[s] - 1:
                last_square.setdefault(s, []).append(square)
            elif h > 0:
                nc.gpsimd.tensor_tensor(
                    out=square_sum[s][:], in0=square_sum[s][:], in1=square[:], op=ALU.add
                )

        def scale_bank(bank):
            acc, scaled = acc_of[bank], scaled_of[bank]
            for head, columns in pieces(bank):
                nc.scalar.activation(
                    out=scaled[:, columns],
                    in_=acc[:, columns],
                    func=ACT.Identity,
                    bias=gain_bias_col[:, head : head + 1],
                    scale=gain_col[:, head : head + 1],
                )

        def turn_back(bank):
            back = back_pool.tile([P, TOKEN_TILES, HEAD_DIM], F32, name="back")
            s, h, heads = BANKS[bank]
            for j in range(heads * SECTIONS[s][2]):
                nc.tensor.transpose(
                    back[:, j, :], scaled_of[bank][:, j * P : (j + 1) * P], ident[:]
                )
            return back

        def rotate(bank, back):
            s, h, heads = BANKS[bank]
            half, first_tile, tiles = SECTIONS[s]
            if h == 0:
                rotated[s] = const.tile([P, tiles, HEADS, HEAD_DIM], F32, name="rotated_%d" % s)
            x = back[:, 0 : heads * tiles, :].rearrange("p (i t) d -> p i t d", i=heads)
            shape = [P, heads, tiles, HEAD_DIM]
            these = slice(first_tile, first_tile + tiles)
            cos_table = cos_f[:, these, :].unsqueeze(1).to_broadcast(shape)
            sin_table = sin_signed[:, these, :].unsqueeze(1).to_broadcast(shape)
            straight = stage.tile(shape, F32, name="straight")
            crossed = stage.tile(shape, F32, name="crossed")
            if s < LAST:
                nc.vector.tensor_tensor(out=straight[:], in0=x, in1=cos_table, op=ALU.mult)
                halves = "p i t (two h) -> p i t two h"
                nc.vector.tensor_tensor(
                    out=crossed[:].rearrange(halves, two=2),
                    in0=x.rearrange(halves, two=2)[:, :, :, ::-1, :],
                    in1=sin_table.rearrange(halves, two=2),
                    op=ALU.mult,
                )
            else:
                low, high = slice(0, HALF_DIM), slice(HALF_DIM, HEAD_DIM)
                for out, source, table in (
                    (straight[:], x, cos_table),
                    (crossed[:, :, :, low], x[:, :, :, high], sin_table[:, :, :, low]),
                    (crossed[:, :, :, high], x[:, :, :, low], sin_table[:, :, :, high]),
                ):
                    nc.vector.scalar_tensor_tensor(
                        out=out,
                        in0=source,
                        scalar=inv_rms_of[s][:, 0:1],
                        in1=table,
                        op0=ALU.mult,
                        op1=ALU.mult,
                    )
            products_of[bank] = (straight, crossed)

        def add_products(bank):
            s, h, heads = BANKS[bank]
            half, first_tile, tiles = SECTIONS[s]
            straight, crossed = products_of[bank]
            engine = nc.gpsimd if s == LAST and bank < len(BANKS) - 1 else nc.vector
            engine.tensor_tensor(
                out=rotated[s][:, :, h : h + heads, :].rearrange("p t i d -> p i t d"),
                in0=straight[:],
                in1=crossed[:],
                op=ALU.add,
            )
            if s == LAST:
                nc.sync.dma_start(
                    out=outs[half][first_tile * P :, h * HEAD_DIM : (h + heads) * HEAD_DIM],
                    in_=rotated[s][:, 0, h : h + heads, :].rearrange("p h d -> p (h d)"),
                )

        def turn_squares(s):
            half, first_tile, tiles = SECTIONS[s]
            heads = BANKS[last_bank_of[s]][2]
            sums_back = back_pool.tile([P, TOKEN_TILES, HEAD_DIM], F32, name="back")
            for j in range(heads * tiles):
                terms = [square_sum[s]] + last_square[s]
                for i, squares in enumerate(terms):
                    nc.tensor.matmul(
                        out=sums_back[:, j, :],
                        lhsT=squares[:, j * P : (j + 1) * P],
                        rhs=ident[:],
                        is_transpose=True,
                        start=(i == 0),
                        stop=(i == len(terms) - 1),
                    )
            return sums_back[:, 0 : heads * tiles, :]

        def turn_squares_of_bank(bank, last_sums):
            s, h, heads = BANKS[bank]
            for i in range(heads):
                nc.tensor.matmul(
                    out=last_sums[:, 0:P],
                    lhsT=square_of[bank][:, i * P : (i + 1) * P],
                    rhs=ident[:],
                    is_transpose=True,
                    start=(h + i == 0),
                    stop=(h + i == HEADS - 1),
                )

        def root_mean_square(s, sums_back):
            half, first_tile, tiles = SECTIONS[s]
            heads = BANKS[last_bank_of[s]][2] if s < LAST else 1
            total = const.tile([P, tiles], F32, name="total_%d" % s)
            by_tile = sums_back.rearrange("p (i t) d -> p t i d", t=tiles)
            unused = stage.tile([P, tiles, heads, HEAD_DIM], F32, name="unused")
            for t in range(tiles):
                nc.scalar.activation(
                    out=unused[:, t, :, :],
                    in_=by_tile[:, t, :, :],
                    func=ACT.Copy,
                    accum_out=total[:, t : t + 1],
                )
            rms = const.tile([P, tiles], F32, name="rms_%d" % s)
            nc.scalar.activation(
                out=rms[:], in_=total[:], func=ACT.Sqrt, bias=eps_col[:, 0:1], scale=1.0 / DIM
            )
            inv_rms = const.tile([P, tiles], F32, name="inv_rms_%d" % s)
            inv_rms_of[s] = inv_rms
            rms_of[s] = rms

        def scale_and_store(s, t, part, engine):
            half, first_tile, tiles = SECTIONS[s]
            heads = slice(part * HEADS // PARTS, (part + 1) * HEADS // PARTS)
            columns = slice(part * DIM // PARTS, (part + 1) * DIM // PARTS)
            row = rotated[s][:, t, heads, :].rearrange("p h d -> p (h d)")
            factor = inv_rms_of[s][:, t : t + 1]
            if engine == "scalar":
                nc.scalar.activation(out=row, in_=row, func=ACT.Copy, scale=factor)
            else:
                nc.vector.tensor_scalar(
                    out=row, in0=row, scalar1=factor, scalar2=None, op0=ALU.mult
                )
            token = (first_tile + t) * P
            nc.sync.dma_start(out=outs[half][token : token + P, columns], in_=row)

        LEAD = 3
        EARLY = 2
        late = [b for b in range(len(BANKS)) if BANKS[b][0] == LAST]
        multiply_at = {b: b + LEAD - (EARLY if b in late else 0) for b in range(len(BANKS))}
        turn_at = {b: b + LEAD + (3 if b in late else 2) for b in range(len(BANKS))}
        rotate_at = {b: turn_at[b] + (1 if b in late else 0) for b in range(len(BANKS))}
        SCALERS = {0: ["vector"], 1: ["vector"] * 3 + ["scalar"] * 3}
        tail = []
        STORES_ONLY = 36
        for step in range(max(rotate_at.values()) + 1):
            multiplied = [b for b in range(len(BANKS)) if multiply_at[b] == step]
            squared = [b for b in range(len(BANKS)) if multiply_at[b] + 1 == step]
            summed = [b for b in late[:-1] if multiply_at[b] + 2 == step]
            turned = [b for b in range(len(BANKS)) if turn_at[b] == step]
            rotated_now = [b for b in range(len(BANKS)) if rotate_at[b] == step]
            done = [
                s
                for s in last_bank_of
                if multiply_at[last_bank_of[s]] + (2 if s == 0 else 1) == step
            ]
            if step + PREFETCH < ALL_HEADS:
                load_weights(step + PREFETCH)
            for b in turned:
                if b not in late:
                    back_of[b] = turn_back(b)
            if 0 <= step - 1 < ALL_HEADS:
                regroup_weights(step - 1)
            for b in squared:
                bias_gain_square(b)
            sums = {s: turn_squares(s) for s in done if s < LAST}
            for b in multiplied:
                multiply(b)
            for b in summed:
                if b == late[0]:
                    last_sums = acc_pool.tile([P, TOKENS], F32, name="acc")
                turn_squares_of_bank(b, last_sums)
            if LAST in done:
                turn_squares_of_bank(late[-1], last_sums)
                sums[LAST] = last_sums[:, 0:P].unsqueeze(1)
            for b in turned:
                if b in late:
                    back_of[b] = turn_back(b)
            if step < ALL_HEADS:
                flip(step)
            if step < LEAD:
                keep_warm()
            for s in done:
                root_mean_square(s, sums[s])
            for b in squared:
                if b in late:
                    scale_bank(b)
            if step >= STORES_ONLY:
                now, tail = tail[:3], tail[3:]
                for piece in now:
                    scale_and_store(*piece)
            if LAST in done:
                nc.vector.reciprocal(out=inv_rms_of[LAST][:], in_=rms_of[LAST][:])
            for b in rotated_now:
                rotate(b, back_of[b])
            if 0 <= step - 2 < ALL_HEADS:
                quantise(step - 2)
            for b in rotated_now:
                add_products(b)
            for s in done:
                if s < LAST:
                    nc.vector.reciprocal(out=inv_rms_of[s][:], in_=rms_of[s][:])
            if step < STORES_ONLY and tail and step % 2 == 0:
                scale_and_store(*tail.pop(0))
            for s in done:
                if s < LAST:
                    order = [(t, part) for part in range(PARTS) for t in range(SECTIONS[s][2])]
                    for i, (t, part) in enumerate(order):
                        tail.append((s, t, part, SCALERS[s][i % len(SCALERS[s])]))
            if step == 3:
                make_bias_and_gain()
            if step == 4:
                make_rope_tables()
